import numpy as np
import ml_dtypes


def mxq(x, axis, fmt="e4m3"):
    dtype, down = {"e4m3": (ml_dtypes.float8_e4m3fn, 7), "e5m2": (ml_dtypes.float8_e5m2, 14)}[fmt]
    v = np.moveaxis(np.asarray(x, np.float32).astype(ml_dtypes.bfloat16).astype(np.float64), axis, -1)
    blocks = v.reshape(v.shape[:-1] + (-1, 32))
    amax = np.abs(blocks).max(-1, keepdims=True)
    byte = np.maximum(np.where(amax > 0, np.frexp(amax)[1] - 1 + 127, 0) - down, 1)
    scale = np.exp2(byte - 127.0)
    codes = (blocks / scale).astype(np.float32).astype(dtype).astype(np.float64)
    return np.moveaxis((codes * scale).reshape(v.shape), -1, axis)


WIDE = False


def mx_kscale(k):
    if not WIDE:
        return np.ones(k)
    levels = np.array([10, -10, 5, -5, 0])
    a = np.random.permutation(np.resize(levels, k // 512 * 4)).reshape(k // 512, 4)
    idx = np.arange(k)
    return np.exp2(a[idx // 512, idx % 128 // 32])


BF16 = ml_dtypes.bfloat16


def bf(x):
    return np.asarray(x, np.float32).astype(BF16)


def f64(x):
    return np.asarray(x).astype(np.float64)


B, H, C, W = 1, 512, 4096, 1024
EPS = 1e-8
MASK_MIN = 0.0


def setup_inputs():
    s = mx_kscale(W)
    rows = 0.5 + 1.5 * np.random.random_sample((B, C, 1))
    return {"memory": bf(np.random.standard_normal((B, C, W)) * rows * s),
            "keys": bf(np.random.standard_normal((B, H, W)) * s),
            "betas": bf(np.sqrt(W) * (0.6 + 0.6 * np.random.random_sample((B, H)))),
            "mask": bf(np.random.random_sample((B, H, W)) / s)}


def reference(memory, keys, betas, mask):
    memory, keys, betas = f64(memory), f64(keys), f64(betas)
    mask = f64(mask) * (1.0 - MASK_MIN) + MASK_MIN
    m2 = mask * mask
    keys_m = keys * mask
    dots = mxq(keys * m2, 2, "e4m3") @ mxq(memory, 2, "e4m3").transpose(0, 2, 1)
    keys_norm = np.sqrt((keys_m * keys_m).sum(-1))
    mem_norm = np.sqrt(mxq(m2, 2, "e4m3") @ mxq(memory * memory, 2, "e4m3").transpose(0, 2, 1))
    norm = keys_norm[..., None] * mem_norm
    scores = dots / (norm + EPS) * betas[..., None]
    e = np.exp(scores - scores.max(-1, keepdims=True))
    return e / e.sum(-1, keepdims=True)

@@ -1,0 +1,357 @@
+from contextlib import ExitStack
+
+import concourse.mybir as mybir
+from concourse.masks import make_identity
+
+F32 = mybir.dt.float32
+BF16 = mybir.dt.bfloat16
+U32 = mybir.dt.uint32
+U8 = mybir.dt.uint8
+FP8X4 = mybir.dt.float8_e4m3fn_x4
+AF = mybir.ActivationFunctionType
+ALU = mybir.AluOpType
+AX = mybir.AxisListType
+
+P = 128
+H, C, W = 512, 4096, 1024
+HT = H // P
+CHUNK = 512
+NCH = C // CHUNK
+G = W // 512
+NPAIR = NCH * HT
+LEAD = 2
+ACT_BLOCKS = (1, 1, 1, 0)
+VEC_RUNS = ((0, 3, 1), (3, 4, 0),)
+EPS = 1e-8
+FLOPS = 2 * 2 * H * C * W
+
+
+def tile_contentaddressing_t_kernel(tc, memory, keys, betas, mask, out):
+    nc = tc.nc
+    mem2d = memory.flatten_outer_dims()
+    keys2d = keys.flatten_outer_dims()
+    mask2d = mask.flatten_outer_dims()
+    out2d = out.flatten_outer_dims()
+
+    with ExitStack() as ctx:
+        const = ctx.enter_context(tc.tile_pool(name="const", bufs=1))
+        natp = ctx.enter_context(tc.tile_pool(name="natp", bufs=3))
+        grp = ctx.enter_context(tc.tile_pool(name="grp", bufs=2))
+        cod = ctx.enter_context(tc.tile_pool(name="cod", bufs=3))
+        wrk = ctx.enter_context(tc.tile_pool(name="wrk", bufs=4))
+        psum = ctx.enter_context(tc.psum_pool(name="psum", bufs=2))
+        ctx.enter_context(tc.manual_schedule())
+
+        tiny = const.tile([P, 1], F32, name="tiny")
+        nc.vector.memset(tiny[:], 1e-30)
+        b1 = const.tile([P, 1], F32, name="b1")
+        nc.vector.memset(b1[:], 1e-16)
+        warm = const.tile([P, 1], F32, name="warm")
+        nc.scalar.activation(out=warm[:], in_=b1[:], func=AF.Abs_reciprocal_sqrt, bias=tiny[:], scale=1.0)
+        brow = const.tile([P, P], BF16, name="brow")
+        nc.vector.memset(brow[:], 0.0)
+        ident_f = const.tile([P, P], F32, name="ident_f")
+        make_identity(nc, ident_f[:])
+        ident_b = const.tile([P, P], BF16, name="ident_b")
+        make_identity(nc, ident_b[:])
+
+        keys_nat = const.tile([P, HT, W], BF16, name="keys_nat")
+        mask_nat = const.tile([P, HT, W], BF16, name="mask_nat")
+        kview = keys2d.rearrange("(t p) w -> p t w", p=P)
+        mview = mask2d.rearrange("(t p) w -> p t w", p=P)
+        nat = {}
+
+        def load_mem(k):
+            t_nat = natp.tile([P, 4, W], BF16, name="mem_nat")
+            nc.sync.dma_start(
+                out=t_nat[:],
+                in_=mem2d[k * CHUNK:(k + 1) * CHUNK, :].rearrange("(j p) w -> p j w", p=P),
+            )
+            nat[k] = t_nat
+
+        nc.scalar.dma_start(out=brow[0:HT, :], in_=betas.rearrange("o (t p) -> (o t) p", p=P))
+        for t in range(HT):
+            nc.sync.dma_start(out=mask_nat[:, t, :], in_=mview[:, t, :])
+            nc.sync.dma_start(out=keys_nat[:, t, :], in_=kview[:, t, :])
+        load_mem(0)
+        load_mem(1)
+        load_mem(2)
+
+        beta_f = const.tile([P, HT], F32, name="beta_f")
+        kn2 = const.tile([P, HT], F32, name="kn2")
+        rk = const.tile([P, HT], F32, name="rk")
+        rk2 = const.tile([P, HT], F32, name="rk2")
+        sc1 = const.tile([P, HT], F32, name="sc1")
+        e2 = const.tile([P, HT], F32, name="e2")
+        bk = const.tile([P, HT], F32, name="bk")
+        kcodes = const.tile([P, HT * 512], U32, name="kcodes", align_bytes=64)
+        kscale = const.tile([P, HT * 512], U8, name="kscale", align_bytes=64)
+        kgrp = [const.tile([P, 2, G, P, 4], BF16, name="kgrp%d" % t, align_bytes=64) for t in range(HT)]
+        s_all = [const.tile([P, C], F32, name="s%d" % t) for t in range(HT)]
+        mxp = const.tile([P, NCH], F32, name="mxp")
+
+        def t_bank(shape, dtype):
+            return psum.tile(shape, dtype, name="tbank", tag="T", bufs=3)
+
+        def acc_bank(op, shape):
+            if op == 0:
+                return psum.tile(shape, F32, name="dots", tag="dots", bufs=3)
+            return psum.tile(shape, F32, name="mn2", tag="mn2", bufs=2)
+
+        bT = t_bank([P, P], BF16)
+        nc.tensor.transpose(out=bT[:], in_=brow[:], identity=ident_b[:])
+        nc.vector.tensor_copy(out=beta_f[:], in_=bT[:, 0:HT])
+
+        perm = "p (a q e) -> p a e q"
+        m2f = [s_all[t][:, 0:W] for t in range(HT)]
+        km2f = [s_all[t][:, W:2 * W] for t in range(HT)]
+        junk = [s_all[t][:, 2 * W:3 * W] for t in range(HT)]
+        kx = {}
+
+        def key_square(t):
+            nc.scalar.activation(out=m2f[t], in_=mask_nat[:, t, :], func=AF.Square)
+
+        def key_products(t):
+            k_t = keys_nat[:, t, :]
+            nc.vector.tensor_tensor(out=km2f[t], in0=k_t, in1=m2f[t], op=ALU.mult)
+            nc.vector.scalar_tensor_tensor(out=junk[t], in0=k_t, scalar=1.0, in1=km2f[t],
+                                           op0=ALU.mult, op1=ALU.mult, accum_out=kn2[:, t:t + 1])
+
+        def key_transposes(t, op):
+            cols = (km2f[t] if op == 0 else m2f[t]).rearrange(perm, a=4, q=P, e=2)
+            for g in range(G):
+                xt = acc_bank(g, [P, 4, P])
+                for u in range(2):
+                    for e in range(2):
+                        nc.tensor.transpose(out=xt[:, 2 * u + e, :], in_=cols[:, 2 * g + u, e, :],
+                                            identity=ident_f[:])
+                kx[(t, op, g)] = xt
+
+        def key_evac(t, op, eng):
+            for g in range(G):
+                src = kx[(t, op, g)][:].rearrange("p s h -> p h s")
+                if eng == "v":
+                    nc.vector.tensor_copy(out=kgrp[t][:, op, g], in_=src)
+                else:
+                    nc.scalar.copy(out=kgrp[t][:, op, g], in_=src)
+
+        def key_quant(t):
+            nc.vector.quantize_mx(
+                out=kcodes[:, t * 512:(t + 1) * 512].bitcast(FP8X4),
+                scales=kscale[:, t * 512:(t + 1) * 512],
+                in_=kgrp[t][:].rearrange("p o g h s -> p (o g h s)"),
+            )
+
+        mp = {}
+
+        def mem_transposes(k, b):
+            g, half = divmod(b, 2)
+            memf = nat[k][:].bitcast(F32)
+            tb = t_bank([P, 2, 256], F32)
+            for jj in range(2):
+                for u in range(2):
+                    i = 2 * g + u
+                    nc.tensor.transpose(
+                        out=tb[:, u, jj * P:(jj + 1) * P],
+                        in_=memf[:, 2 * half + jj, i * P:(i + 1) * P],
+                        identity=ident_f[:])
+            mp[(k, "tb", b)] = tb
+
+        def mem_tiles(k):
+            mp[(k, "mgrp")] = grp.tile([P, G, CHUNK, 4], BF16, name="mgrp", align_bytes=64)
+            mp[(k, "msq")] = grp.tile([P, G, CHUNK, 4], BF16, name="msq", align_bytes=64)
+
+        def mem_evac(k, b):
+            g, half = divmod(b, 2)
+            tb = mp[(k, "tb", b)]
+            nc.scalar.copy(out=mp[(k, "mgrp")][:].bitcast(F32)[:, g, 256 * half:256 * half + 256, :],
+                           in_=tb[:].rearrange("p u r -> p r u"))
+            n_act = ACT_BLOCKS[b] * P
+            if n_act:
+                nc.scalar.activation(
+                    out=mp[(k, "msq")][:, g, 256 * half:256 * half + n_act, :].rearrange("p r (u e) -> p r u e", e=2),
+                    in_=tb[:, :, 0:n_act].bitcast(BF16).rearrange("p u (r e) -> p r u e", e=2),
+                    func=AF.Square)
+
+        def mem_square_vec(k):
+            view = "p g (h j c) s -> p (g h) j (c s)"
+            src = mp[(k, "mgrp")][:].rearrange(view, h=2, j=2, c=P)
+            dst = mp[(k, "msq")][:].rearrange(view, h=2, j=2, c=P)
+            for b0, b1, j0 in VEC_RUNS:
+                nc.vector.tensor_tensor(out=dst[:, b0:b1, j0:2, :], in0=src[:, b0:b1, j0:2, :],
+                                        in1=src[:, b0:b1, j0:2, :], op=ALU.mult)
+
+        def quant(k, which):
+            dat = cod.tile([P, G * CHUNK], U32, name="dat_" + which, align_bytes=64)
+            scl = cod.tile([P, G * CHUNK], U8, name="scl_" + which, align_bytes=64)
+            nc.vector.quantize_mx(out=dat[:].bitcast(FP8X4), scales=scl[:],
+                                  in_=mp[(k, which)][:].rearrange("p g c s -> p (g c s)"))
+            mp[(k, "q", which)] = (dat, scl)
+
+        pr = {}
+
+        def product(n, op):
+            k, t = divmod(n, HT)
+            acc = acc_bank(op, [P, CHUNK])
+            dat, scl = mp[(k, "q", "mgrp" if op == 0 else "msq")]
+            for g in range(G):
+                c0 = t * 512 + (op * G + g) * P
+                nc.tensor.matmul_mx(
+                    out=acc[:],
+                    lhsT=kcodes[:, c0:c0 + P].bitcast(FP8X4),
+                    lhsT_scale=kscale[:, c0:c0 + P],
+                    rhs=dat[:, g * CHUNK:(g + 1) * CHUNK].bitcast(FP8X4),
+                    rhs_scale=scl[:, g * CHUNK:(g + 1) * CHUNK],
+                    start=(g == 0), stop=(g == G - 1))
+            pr[(n, op)] = acc
+
+        def a1(n):
+            t = n % HT
+            w = wrk.tile([P, CHUNK], F32, name="w")
+            nc.scalar.activation(out=w[:], in_=pr[(n, 1)][:], func=AF.Abs_reciprocal_sqrt,
+                                 bias=b1[:], scale=sc1[:, t:t + 1])
+            pr[(n, "w")] = w
+
+        def v1(n):
+            w = pr[(n, "w")]
+            nc.vector.scalar_tensor_tensor(out=w[:], in0=w[:], scalar=1.0, in1=pr[(n, 1)][:],
+                                           op0=ALU.add, op1=ALU.mult)
+
+        def a2(n):
+            t = n % HT
+            w = pr[(n, "w")]
+            nc.scalar.activation(out=w[:], in_=w[:], func=AF.Abs_reciprocal_sqrt,
+                                 bias=e2[:, t:t + 1], scale=1.0)
+
+        def v2(n):
+            k, t = divmod(n, HT)
+            nc.vector.scalar_tensor_tensor(out=s_all[t][:, k * CHUNK:(k + 1) * CHUNK], in0=pr[(n, 0)][:],
+                                           scalar=bk[:, t:t + 1], in1=pr[(n, "w")][:],
+                                           op0=ALU.mult, op1=ALU.mult)
+
+        def max0(k):
+            nc.vector.tensor_reduce(out=mxp[:, k:k + 1], in_=s_all[0][:, k * CHUNK:(k + 1) * CHUNK],
+                                    axis=AX.X, op=ALU.max)
+
+        def mem_first(k):
+            mem_tiles(k)
+            for b in range(4):
+                mem_transposes(k, b)
+                mem_evac(k, b)
+
+        for t in range(HT):
+            key_square(t)
+        key_products(0)
+        key_transposes(0, 1)
+        key_transposes(1, 1)
+        key_evac(0, 1, "a")
+        key_evac(1, 1, "a")
+        key_products(1)
+        key_transposes(2, 1)
+        key_transposes(3, 1)
+        key_evac(2, 1, "a")
+        key_evac(3, 1, "a")
+        key_products(2)
+        key_transposes(0, 0)
+        key_transposes(1, 0)
+        key_evac(0, 0, "a")
+        key_evac(1, 0, "a")
+        key_products(3)
+        nc.scalar.activation(out=rk[:], in_=kn2[:], func=AF.Abs_reciprocal_sqrt, bias=tiny[:], scale=1.0)
+        key_transposes(2, 0)
+        key_transposes(3, 0)
+        mem_first(0)
+        key_evac(2, 0, "v")
+        key_quant(0)
+        key_evac(3, 0, "v")
+        key_quant(1)
+        key_quant(2)
+        key_quant(3)
+        nc.vector.tensor_scalar(out=sc1[:], in0=kn2[:], scalar1=1.0 / (4.0 * EPS * EPS),
+                                scalar2=3e38, op0=ALU.mult, op1=ALU.min)
+        nc.vector.tensor_tensor(out=rk2[:], in0=rk[:], in1=rk[:], op=ALU.mult)
+        nc.vector.tensor_scalar(out=e2[:], in0=rk2[:], scalar1=EPS * EPS,
+                                scalar2=1e-37, op0=ALU.mult, op1=ALU.max)
+        nc.vector.tensor_tensor(out=bk[:], in0=beta_f[:], in1=rk[:], op=ALU.mult)
+        mem_square_vec(0)
+        quant(0, "msq")
+        mem_first(1)
+        product(0, 1)
+        quant(0, "mgrp")
+        product(0, 0)
+        for b in range(LEAD):
+            mem_transposes(2, b)
+
+        for n in range(NPAIR + 1):
+            k, j = divmod(n, HT)
+            if j == 0 and k + 3 < NCH:
+                load_mem(k + 3)
+            if n + 1 < NPAIR:
+                product(n + 1, 1)
+            if n < NPAIR:
+                a1(n)
+                v1(n)
+            if n >= 1:
+                a2(n - 1)
+                v2(n - 1)
+            if n + 1 < NPAIR:
+                product(n + 1, 0)
+            ka, ba = divmod(n + LEAD, HT)
+            if ka + 2 < NCH:
+                mem_transposes(ka + 2, ba)
+            if k + 2 < NCH:
+                if j == 0:
+                    mem_tiles(k + 2)
+                mem_evac(k + 2, j)
+            if k + 1 < NCH:
+                if j == 0:
+                    mem_square_vec(k + 1)
+                elif j == 1:
+                    quant(k + 1, "msq")
+                elif j == 2:
+                    quant(k + 1, "mgrp")
+            if j == 3:
+                max0(k)
+
+        negm = [const.tile([P, 1], F32, name="negm%d" % t) for t in range(HT)]
+        mrow = [const.tile([P, 1], F32, name="mrow%d" % t) for t in range(HT)]
+        sums = [const.tile([P, 1], F32, name="sums%d" % t) for t in range(HT)]
+        rs = [const.tile([P, 1], F32, name="rs%d" % t) for t in range(HT)]
+
+        def row_max(t):
+            nc.vector.tensor_reduce(out=mrow[t][:], in_=(mxp[:] if t == 0 else s_all[t][:]), axis=AX.X, op=ALU.max)
+            nc.vector.tensor_scalar(out=negm[t][:], in0=mrow[t][:], scalar1=-1.0, scalar2=None, op0=ALU.mult)
+
+        def row_exp(t):
+            nc.scalar.activation(out=s_all[t][:], in_=s_all[t][:], func=AF.Exp,
+                                 bias=negm[t][:], scale=1.0, accum_out=sums[t][:])
+
+        def row_recip(t):
+            nc.vector.reciprocal(out=rs[t][:], in_=sums[t][:])
+
+        def row_scale_store(t, q, eng):
+            cs = slice(q * 1024, (q + 1) * 1024)
+            piece = s_all[t][:, cs]
+            if eng == "v":
+                nc.vector.tensor_scalar(out=piece, in0=piece, scalar1=rs[t][:], scalar2=None, op0=ALU.mult)
+            elif eng == "a":
+                nc.scalar.activation(out=piece, in_=piece, func=AF.Copy, scale=rs[t][:])
+            else:
+                nc.gpsimd.tensor_scalar(out=piece, in0=piece, scalar1=rs[t][:], scalar2=0.0,
+                                        op0=ALU.mult, op1=ALU.add)
+            nc.sync.dma_start(out=out2d[t * P:(t + 1) * P, cs], in_=piece)
+
+        row_max(0)
+        row_exp(0)
+        row_max(1)
+        for t in range(HT):
+            if t + 1 < HT:
+                row_exp(t + 1)
+            row_recip(t)
+            last = t == HT - 1
+            row_scale_store(t, 0, "v")
+            row_scale_store(t, 1, "v" if last else "g")
+            row_scale_store(t, 2, "a" if last else "g")
+            row_scale_store(t, 3, "g")
+            if t + 2 < HT:
+                row_max(t + 2)

@@ -18,12 +18,23 @@ HT = H // P
 CHUNK = 512
 NCH = C // CHUNK
 G = W // 512
-NPAIR = NCH * HT
-LEAD = 2
-ACT_BLOCKS = (1, 1, 1, 0)
-VEC_RUNS = ((0, 3, 1), (3, 4, 0),)
+PIECE = 1024
+NQ = C // PIECE
+S_SQ = (0, 1)
+RECIP = (None, (3, 0), (3, 2))
+ENG1 = "ggvv"
+NAT_BUFS = 2
+S_FROM = 0
+DEFER = 5
+S_CELLS = 0
+S_KEVAC = (1, 2, 3)
+ENG2 = "ggvv"
 EPS = 1e-8
 FLOPS = 2 * 2 * H * C * W
+
+
+def s_cells(k):
+    return S_CELLS if k >= S_FROM else 0
 
 
 def tile_contentaddressing_t_kernel(tc, memory, keys, betas, mask, out):
@@ -35,114 +46,124 @@ def tile_contentaddressing_t_kernel(tc, memory, keys, betas, mask, out):
 
     with ExitStack() as ctx:
         const = ctx.enter_context(tc.tile_pool(name="const", bufs=1))
-        natp = ctx.enter_context(tc.tile_pool(name="natp", bufs=3))
+        natp = ctx.enter_context(tc.tile_pool(name="natp", bufs=NAT_BUFS))
         grp = ctx.enter_context(tc.tile_pool(name="grp", bufs=2))
+        memp = ctx.enter_context(tc.tile_pool(name="memp", bufs=NCH - DEFER))
         cod = ctx.enter_context(tc.tile_pool(name="cod", bufs=3))
-        wrk = ctx.enter_context(tc.tile_pool(name="wrk", bufs=4))
-        psum = ctx.enter_context(tc.psum_pool(name="psum", bufs=2))
+        psum = ctx.enter_context(tc.psum_pool(name="psum", bufs=4))
         ctx.enter_context(tc.manual_schedule())
 
-        tiny = const.tile([P, 1], F32, name="tiny")
-        nc.vector.memset(tiny[:], 1e-30)
-        b1 = const.tile([P, 1], F32, name="b1")
-        nc.vector.memset(b1[:], 1e-16)
+        b_tiny = const.tile([P, 1], F32, name="b_tiny")
+        nc.vector.memset(b_tiny[:], 1e-34)
+        b_eps = const.tile([P, 1], F32, name="b_eps")
+        nc.vector.memset(b_eps[:], EPS)
         warm = const.tile([P, 1], F32, name="warm")
-        nc.scalar.activation(out=warm[:], in_=b1[:], func=AF.Abs_reciprocal_sqrt, bias=tiny[:], scale=1.0)
+        nc.scalar.activation(out=warm[:], in_=b_eps[:], func=AF.Sqrt, bias=b_tiny[:], scale=1.0)
         brow = const.tile([P, P], BF16, name="brow")
         nc.vector.memset(brow[:], 0.0)
         ident_f = const.tile([P, P], F32, name="ident_f")
         make_identity(nc, ident_f[:])
         ident_b = const.tile([P, P], BF16, name="ident_b")
-        make_identity(nc, ident_b[:])
+        nc.vector.tensor_copy(out=ident_b[:], in_=ident_f[:])
 
-        keys_nat = const.tile([P, HT, W], BF16, name="keys_nat")
-        mask_nat = const.tile([P, HT, W], BF16, name="mask_nat")
-        kview = keys2d.rearrange("(t p) w -> p t w", p=P)
-        mview = mask2d.rearrange("(t p) w -> p t w", p=P)
+        keys_nat = [const.tile([P, W], BF16, name="keys_nat%d" % t) for t in range(HT)]
+        mask_nat = [const.tile([P, W], BF16, name="mask_nat%d" % t) for t in range(HT)]
         nat = {}
+
+        def load_head(dst, src, t):
+            nc.sync.dma_start(out=dst[t][:], in_=src[t * P:(t + 1) * P, :])
 
         def load_mem(k):
             t_nat = natp.tile([P, 4, W], BF16, name="mem_nat")
-            nc.sync.dma_start(
-                out=t_nat[:],
-                in_=mem2d[k * CHUNK:(k + 1) * CHUNK, :].rearrange("(j p) w -> p j w", p=P),
-            )
+            view = mem2d[k * CHUNK:(k + 1) * CHUNK, :].rearrange("(j p) w -> p j w", p=P)
+            for j in range(0, 4, 2):
+                nc.sync.dma_start(out=t_nat[:, j:j + 2, :], in_=view[:, j:j + 2, :])
             nat[k] = t_nat
 
         nc.scalar.dma_start(out=brow[0:HT, :], in_=betas.rearrange("o (t p) -> (o t) p", p=P))
-        for t in range(HT):
-            nc.sync.dma_start(out=mask_nat[:, t, :], in_=mview[:, t, :])
-            nc.sync.dma_start(out=keys_nat[:, t, :], in_=kview[:, t, :])
+        for t in range(2):
+            load_head(mask_nat, mask2d, t)
+            load_head(keys_nat, keys2d, t)
         load_mem(0)
+        for t in range(2, HT):
+            load_head(mask_nat, mask2d, t)
         load_mem(1)
-        load_mem(2)
+        for t in range(2, HT):
+            load_head(keys_nat, keys2d, t)
 
         beta_f = const.tile([P, HT], F32, name="beta_f")
         kn2 = const.tile([P, HT], F32, name="kn2")
-        rk = const.tile([P, HT], F32, name="rk")
-        rk2 = const.tile([P, HT], F32, name="rk2")
-        sc1 = const.tile([P, HT], F32, name="sc1")
-        e2 = const.tile([P, HT], F32, name="e2")
-        bk = const.tile([P, HT], F32, name="bk")
+        kn = const.tile([P, HT], F32, name="kn")
+        junk = const.tile([P, P], F32, name="junk")
         kcodes = const.tile([P, HT * 512], U32, name="kcodes", align_bytes=64)
         kscale = const.tile([P, HT * 512], U8, name="kscale", align_bytes=64)
-        kgrp = [const.tile([P, 2, G, P, 4], BF16, name="kgrp%d" % t, align_bytes=64) for t in range(HT)]
+        mask_grp = [const.tile([P, G, P, 4], BF16, name="mask_grp%d" % t, align_bytes=64) for t in range(HT)]
         s_all = [const.tile([P, C], F32, name="s%d" % t) for t in range(HT)]
-        mxp = const.tile([P, NCH], F32, name="mxp")
+        mem_codes = [const.tile([P, G * CHUNK], U32, name="mem_codes%d" % k, align_bytes=64) for k in range(NCH)]
+        mem_scale = [const.tile([P, G * CHUNK], U8, name="mem_scale%d" % k, align_bytes=64) for k in range(NCH)]
+        mp = {}
 
         def t_bank(shape, dtype):
-            return psum.tile(shape, dtype, name="tbank", tag="T", bufs=3)
+            return psum.tile(shape, dtype, name="tbank", tag="T")
 
-        def acc_bank(op, shape):
-            if op == 0:
-                return psum.tile(shape, F32, name="dots", tag="dots", bufs=3)
-            return psum.tile(shape, F32, name="mn2", tag="mn2", bufs=2)
+        def acc_bank(shape):
+            return psum.tile(shape, F32, name="acc", tag="acc")
 
-        bT = t_bank([P, P], BF16)
-        nc.tensor.transpose(out=bT[:], in_=brow[:], identity=ident_b[:])
-        nc.vector.tensor_copy(out=beta_f[:], in_=bT[:, 0:HT])
+        flat = "p g h s -> p (g h s)"
 
-        perm = "p (a q e) -> p a e q"
-        m2f = [s_all[t][:, 0:W] for t in range(HT)]
-        km2f = [s_all[t][:, W:2 * W] for t in range(HT)]
-        junk = [s_all[t][:, 2 * W:3 * W] for t in range(HT)]
-        kx = {}
+        def head_transposes(t, src):
+            words = (mask_nat if src == 1 else keys_nat)[t][:].bitcast(F32)
+            xt = acc_bank([P, 2 * G, P])
+            for i in range(2 * G):
+                nc.tensor.transpose(out=xt[:, i, :], in_=words[:, i * P:(i + 1) * P], identity=ident_f[:])
+            mp[("x", t, src)] = xt
+
+        def mask_prep(t):
+            xt = mp[("x", t, 1)]
+            nc.scalar.copy(out=mask_grp[t][:].bitcast(F32), in_=xt[:].rearrange("p (g u) h -> p g h u", u=2))
+            m2 = grp.tile([P, G, P, 4], BF16, name="m2_grp", bufs=HT, align_bytes=64)
+            for g in range(G):
+                nc.scalar.activation(
+                    out=m2[:, g].rearrange("p h (u e) -> p h u e", e=2),
+                    in_=xt[:, 2 * g:2 * g + 2, :].bitcast(BF16).rearrange("p u (h e) -> p h u e", e=2),
+                    func=AF.Square)
+            mp[("q", t, 1)] = m2
+
+        def key_evac(t):
+            xt = mp[("x", t, 0)]
+            kg = grp.tile([P, G, P, 4], BF16, name="keys_grp", align_bytes=64)
+            copy = nc.scalar.copy if t in S_KEVAC else nc.vector.tensor_copy
+            copy(out=kg[:].bitcast(F32), in_=xt[:].rearrange("p (g u) h -> p g h u", u=2))
+            mp[("kg", t)] = kg
+
+        def key_prep(t):
+            kg = mp[("kg", t)]
+            km = grp.tile([P, G, P, 4], F32, name="km")
+            nc.vector.tensor_tensor(out=km[:].rearrange(flat), in0=kg[:].rearrange(flat),
+                                    in1=mask_grp[t][:].rearrange(flat), op=ALU.mult)
+            mp[("km", t)] = km
 
         def key_square(t):
-            nc.scalar.activation(out=m2f[t], in_=mask_nat[:, t, :], func=AF.Square)
+            km2 = grp.tile([P, G, P, 4], BF16, name="km2_grp", align_bytes=64)
+            nc.vector.tensor_tensor(out=km2[:].rearrange(flat), in0=mp[("km", t)][:].rearrange(flat),
+                                    in1=mask_grp[t][:].rearrange(flat), op=ALU.mult)
+            mp[("q", t, 0)] = km2
 
-        def key_products(t):
-            k_t = keys_nat[:, t, :]
-            nc.vector.tensor_tensor(out=km2f[t], in0=k_t, in1=m2f[t], op=ALU.mult)
-            nc.vector.scalar_tensor_tensor(out=junk[t], in0=k_t, scalar=1.0, in1=km2f[t],
+        def head_quant(t, op):
+            cs = slice(t * 512 + op * 256, t * 512 + op * 256 + 256)
+            nc.vector.quantize_mx(out=kcodes[:, cs].bitcast(FP8X4), scales=kscale[:, cs],
+                                  in_=mp[("q", t, op)][:].rearrange(flat))
+
+        def key_gram(t):
+            gram = acc_bank([P, P])
+            for i in range(4 * G):
+                col = mp[("km", t)][:, i // 4, :, i % 4]
+                nc.tensor.matmul(out=gram[:], lhsT=col, rhs=col, start=(i == 0), stop=(i == 4 * G - 1))
+            mp[("gram", t)] = gram
+
+        def key_norm2(t):
+            nc.vector.scalar_tensor_tensor(out=junk[:], in0=mp[("gram", t)][:], scalar=1.0, in1=ident_f[:],
                                            op0=ALU.mult, op1=ALU.mult, accum_out=kn2[:, t:t + 1])
-
-        def key_transposes(t, op):
-            cols = (km2f[t] if op == 0 else m2f[t]).rearrange(perm, a=4, q=P, e=2)
-            for g in range(G):
-                xt = acc_bank(g, [P, 4, P])
-                for u in range(2):
-                    for e in range(2):
-                        nc.tensor.transpose(out=xt[:, 2 * u + e, :], in_=cols[:, 2 * g + u, e, :],
-                                            identity=ident_f[:])
-                kx[(t, op, g)] = xt
-
-        def key_evac(t, op, eng):
-            for g in range(G):
-                src = kx[(t, op, g)][:].rearrange("p s h -> p h s")
-                if eng == "v":
-                    nc.vector.tensor_copy(out=kgrp[t][:, op, g], in_=src)
-                else:
-                    nc.scalar.copy(out=kgrp[t][:, op, g], in_=src)
-
-        def key_quant(t):
-            nc.vector.quantize_mx(
-                out=kcodes[:, t * 512:(t + 1) * 512].bitcast(FP8X4),
-                scales=kscale[:, t * 512:(t + 1) * 512],
-                in_=kgrp[t][:].rearrange("p o g h s -> p (o g h s)"),
-            )
-
-        mp = {}
 
         def mem_transposes(k, b):
             g, half = divmod(b, 2)
@@ -157,45 +178,38 @@ def tile_contentaddressing_t_kernel(tc, memory, keys, betas, mask, out):
                         identity=ident_f[:])
             mp[(k, "tb", b)] = tb
 
-        def mem_tiles(k):
-            mp[(k, "mgrp")] = grp.tile([P, G, CHUNK, 4], BF16, name="mgrp", align_bytes=64)
-            mp[(k, "msq")] = grp.tile([P, G, CHUNK, 4], BF16, name="msq", align_bytes=64)
-
         def mem_evac(k, b):
             g, half = divmod(b, 2)
-            tb = mp[(k, "tb", b)]
-            nc.scalar.copy(out=mp[(k, "mgrp")][:].bitcast(F32)[:, g, 256 * half:256 * half + 256, :],
-                           in_=tb[:].rearrange("p u r -> p r u"))
-            n_act = ACT_BLOCKS[b] * P
-            if n_act:
+            if b == BANKS[0]:
+                mp[(k, "mem")] = memp.tile([P, G, CHUNK, 4], BF16, name="mem_grp", align_bytes=64)
+                mp[(k, "sq")] = grp.tile([P, G, CHUNK, 4], BF16, name="sq_grp", align_bytes=64)
+            nc.scalar.copy(out=mp[(k, "mem")][:].bitcast(F32)[:, g, 256 * half:256 * half + 256, :],
+                           in_=mp[(k, "tb", b)][:].rearrange("p u r -> p r u"))
+            n = s_cells(k)
+            if b == 0 and n:
                 nc.scalar.activation(
-                    out=mp[(k, "msq")][:, g, 256 * half:256 * half + n_act, :].rearrange("p r (u e) -> p r u e", e=2),
-                    in_=tb[:, :, 0:n_act].bitcast(BF16).rearrange("p u (r e) -> p r u e", e=2),
+                    out=mp[(k, "sq")][:, 0, 0:n, :].rearrange("p r (u e) -> p r u e", e=2),
+                    in_=mp[(k, "tb", b)][:, :, 0:n].bitcast(BF16).rearrange("p u (r e) -> p r u e", e=2),
                     func=AF.Square)
 
-        def mem_square_vec(k):
-            view = "p g (h j c) s -> p (g h) j (c s)"
-            src = mp[(k, "mgrp")][:].rearrange(view, h=2, j=2, c=P)
-            dst = mp[(k, "msq")][:].rearrange(view, h=2, j=2, c=P)
-            for b0, b1, j0 in VEC_RUNS:
-                nc.vector.tensor_tensor(out=dst[:, b0:b1, j0:2, :], in0=src[:, b0:b1, j0:2, :],
-                                        in1=src[:, b0:b1, j0:2, :], op=ALU.mult)
+        def mem_square(k):
+            m = mp[(k, "mem")][:].rearrange(flat)[:, 4 * s_cells(k):]
+            nc.vector.tensor_tensor(out=mp[(k, "sq")][:].rearrange(flat)[:, 4 * s_cells(k):], in0=m, in1=m, op=ALU.mult)
 
-        def quant(k, which):
-            dat = cod.tile([P, G * CHUNK], U32, name="dat_" + which, align_bytes=64)
-            scl = cod.tile([P, G * CHUNK], U8, name="scl_" + which, align_bytes=64)
-            nc.vector.quantize_mx(out=dat[:].bitcast(FP8X4), scales=scl[:],
-                                  in_=mp[(k, which)][:].rearrange("p g c s -> p (g c s)"))
-            mp[(k, "q", which)] = (dat, scl)
+        def mem_quant(k):
+            nc.vector.quantize_mx(out=mem_codes[k][:].bitcast(FP8X4), scales=mem_scale[k][:],
+                                  in_=mp[(k, "mem")][:].rearrange(flat))
 
-        pr = {}
+        def sq_quant(k):
+            dat = cod.tile([P, G * CHUNK], U32, name="sq_codes", align_bytes=64)
+            scl = cod.tile([P, G * CHUNK], U8, name="sq_scale", align_bytes=64)
+            nc.vector.quantize_mx(out=dat[:].bitcast(FP8X4), scales=scl[:], in_=mp[(k, "sq")][:].rearrange(flat))
+            mp[(k, "sqq")] = (dat, scl)
 
-        def product(n, op):
-            k, t = divmod(n, HT)
-            acc = acc_bank(op, [P, CHUNK])
-            dat, scl = mp[(k, "q", "mgrp" if op == 0 else "msq")]
+        def product(t, k, op, acc):
+            dat, scl = (mem_codes[k], mem_scale[k]) if op == 0 else mp[(k, "sqq")]
             for g in range(G):
-                c0 = t * 512 + (op * G + g) * P
+                c0 = t * 512 + op * 256 + g * P
                 nc.tensor.matmul_mx(
                     out=acc[:],
                     lhsT=kcodes[:, c0:c0 + P].bitcast(FP8X4),
@@ -203,155 +217,190 @@ def tile_contentaddressing_t_kernel(tc, memory, keys, betas, mask, out):
                     rhs=dat[:, g * CHUNK:(g + 1) * CHUNK].bitcast(FP8X4),
                     rhs_scale=scl[:, g * CHUNK:(g + 1) * CHUNK],
                     start=(g == 0), stop=(g == G - 1))
-            pr[(n, op)] = acc
+            return acc
 
-        def a1(n):
-            t = n % HT
-            w = wrk.tile([P, CHUNK], F32, name="w")
-            nc.scalar.activation(out=w[:], in_=pr[(n, 1)][:], func=AF.Abs_reciprocal_sqrt,
-                                 bias=b1[:], scale=sc1[:, t:t + 1])
-            pr[(n, "w")] = w
+        def chunk_cols(k):
+            return slice(k * CHUNK, (k + 1) * CHUNK)
 
-        def v1(n):
-            w = pr[(n, "w")]
-            nc.vector.scalar_tensor_tensor(out=w[:], in0=w[:], scalar=1.0, in1=pr[(n, 1)][:],
-                                           op0=ALU.add, op1=ALU.mult)
+        def norm_root(t, k):
+            nc.scalar.activation(out=s_all[t][:, chunk_cols(k)], in_=mp[("mn2", t, k)][:], func=AF.Sqrt,
+                                 bias=b_tiny[:], scale=1.0)
 
-        def a2(n):
-            t = n % HT
-            w = pr[(n, "w")]
-            nc.scalar.activation(out=w[:], in_=w[:], func=AF.Abs_reciprocal_sqrt,
-                                 bias=e2[:, t:t + 1], scale=1.0)
+        BANKS = (0, 2, 1, 3)
 
-        def v2(n):
-            k, t = divmod(n, HT)
-            nc.vector.scalar_tensor_tensor(out=s_all[t][:, k * CHUNK:(k + 1) * CHUNK], in0=pr[(n, 0)][:],
-                                           scalar=bk[:, t:t + 1], in1=pr[(n, "w")][:],
+        for t in range(2):
+            head_transposes(t, 1)
+            head_transposes(t, 0)
+        for b in BANKS:
+            mem_transposes(0, b)
+        mask_prep(0)
+        key_evac(0)
+        key_prep(0)
+        key_evac(1)
+        mask_prep(1)
+        head_transposes(2, 1)
+        bT = acc_bank([P, P])
+        nc.tensor.transpose(out=bT[:].bitcast(BF16)[:, 0:P], in_=brow[:], identity=ident_b[:])
+        for b in BANKS:
+            mem_evac(0, b)
+        head_transposes(3, 1)
+        key_prep(1)
+        nc.vector.tensor_copy(out=beta_f[:], in_=bT[:].bitcast(BF16)[:, 0:HT])
+        for b in BANKS:
+            mem_transposes(1, b)
+        key_square(0)
+        head_quant(0, 1)
+        head_quant(1, 1)
+        mask_prep(2)
+        mask_prep(3)
+        mem_square(0)
+        sq_quant(0)
+        head_quant(2, 1)
+        head_quant(3, 1)
+        mem_quant(0)
+        for b in BANKS:
+            mem_evac(1, b)
+        key_square(1)
+
+        for k in range(NCH):
+            if k + 2 < NCH:
+                load_mem(k + 2)
+            if k in (0, 1):
+                head_transposes(k + 2, 0)
+            for t in range(HT):
+                mp[("mn2", t, k)] = product(t, k, 1, acc_bank([P, CHUNK]))
+                norm_root(t, k)
+            if k + 1 < NCH:
+                mem_square(k + 1)
+                sq_quant(k + 1)
+                if k + 1 < DEFER:
+                    mem_quant(k + 1)
+            if k + 2 < NCH:
+                for b in BANKS:
+                    mem_transposes(k + 2, b)
+                for b in BANKS:
+                    mem_evac(k + 2, b)
+            if k in (0, 1, 2, 3):
+                key_gram(k)
+            if k == 2:
+                head_quant(0, 0)
+                head_quant(1, 0)
+            if k in (0, 1):
+                key_evac(k + 2)
+            if k in (1, 2):
+                key_prep(k + 1)
+            if k in (0, 1, 2, 3):
+                key_norm2(k)
+        nc.scalar.activation(out=kn[:], in_=kn2[:], func=AF.Sqrt, bias=b_tiny[:], scale=1.0)
+        for k in range(DEFER, NCH):
+            mem_quant(k)
+        for t in (2, 3):
+            key_square(t)
+            head_quant(t, 0)
+
+        HALF = C // 2
+        last = HT - 1
+        pmx = [const.tile([P, NQ], F32, name="pmx%d" % t) for t in range(HT)]
+        negm = [const.tile([P, 2], F32, name="negm%d" % t) for t in range(HT)]
+        mrow = [const.tile([P, 2], F32, name="mrow%d" % t) for t in range(HT)]
+        sums = [const.tile([P, 1], F32, name="sums%d" % t) for t in range(HT)]
+        sums_a = const.tile([P, 1], F32, name="sums_a")
+        fold = const.tile([P, 1], F32, name="fold")
+        rs = [const.tile([P, 1], F32, name="rs%d" % t) for t in range(HT)]
+        rs_a = const.tile([P, 1], F32, name="rs_a")
+
+        def piece(t, q):
+            return s_all[t][:, q * PIECE:(q + 1) * PIECE]
+
+        def root_recip(i):
+            t, q = divmod(i, NQ)
+            nc.scalar.activation(out=piece(t, q), in_=piece(t, q), func=AF.Abs_reciprocal_sqrt,
+                                 bias=b_eps[:], scale=kn[:, t:t + 1])
+
+        def recip_square(i):
+            t, q = divmod(i, NQ)
+            if i in S_SQ:
+                nc.scalar.activation(out=piece(t, q), in_=piece(t, q), func=AF.Square)
+            else:
+                nc.gpsimd.tensor_tensor(out=piece(t, q), in0=piece(t, q), in1=piece(t, q), op=ALU.mult)
+
+        def score(t, k):
+            bank = acc_bank([P, CHUNK]) if k % 2 == 0 else t_bank([P, CHUNK], F32)
+            product(t, k, 0, bank)
+            col = s_all[t][:, chunk_cols(k)]
+            nc.vector.scalar_tensor_tensor(out=col, in0=bank[:], scalar=beta_f[:, t:t + 1], in1=col,
                                            op0=ALU.mult, op1=ALU.mult)
 
-        def max0(k):
-            nc.vector.tensor_reduce(out=mxp[:, k:k + 1], in_=s_all[0][:, k * CHUNK:(k + 1) * CHUNK],
-                                    axis=AX.X, op=ALU.max)
+        def part_max(t, q):
+            nc.vector.tensor_reduce(out=pmx[t][:, q:q + 1], in_=piece(t, q), axis=AX.X, op=ALU.max)
 
-        def mem_first(k):
-            mem_tiles(k)
-            for b in range(4):
-                mem_transposes(k, b)
-                mem_evac(k, b)
+        def row_max(t, col, nq):
+            nc.vector.tensor_reduce(out=mrow[t][:, col:col + 1], in_=pmx[t][:, 0:nq], axis=AX.X, op=ALU.max)
 
-        for t in range(HT):
-            key_square(t)
-        key_products(0)
-        key_transposes(0, 1)
-        key_transposes(1, 1)
-        key_evac(0, 1, "a")
-        key_evac(1, 1, "a")
-        key_products(1)
-        key_transposes(2, 1)
-        key_transposes(3, 1)
-        key_evac(2, 1, "a")
-        key_evac(3, 1, "a")
-        key_products(2)
-        key_transposes(0, 0)
-        key_transposes(1, 0)
-        key_evac(0, 0, "a")
-        key_evac(1, 0, "a")
-        key_products(3)
-        nc.scalar.activation(out=rk[:], in_=kn2[:], func=AF.Abs_reciprocal_sqrt, bias=tiny[:], scale=1.0)
-        key_transposes(2, 0)
-        key_transposes(3, 0)
-        mem_first(0)
-        key_evac(2, 0, "v")
-        key_quant(0)
-        key_evac(3, 0, "v")
-        key_quant(1)
-        key_quant(2)
-        key_quant(3)
-        nc.vector.tensor_scalar(out=sc1[:], in0=kn2[:], scalar1=1.0 / (4.0 * EPS * EPS),
-                                scalar2=3e38, op0=ALU.mult, op1=ALU.min)
-        nc.vector.tensor_tensor(out=rk2[:], in0=rk[:], in1=rk[:], op=ALU.mult)
-        nc.vector.tensor_scalar(out=e2[:], in0=rk2[:], scalar1=EPS * EPS,
-                                scalar2=1e-37, op0=ALU.mult, op1=ALU.max)
-        nc.vector.tensor_tensor(out=bk[:], in0=beta_f[:], in1=rk[:], op=ALU.mult)
-        mem_square_vec(0)
-        quant(0, "msq")
-        mem_first(1)
-        product(0, 1)
-        quant(0, "mgrp")
-        product(0, 0)
-        for b in range(LEAD):
-            mem_transposes(2, b)
+        def row_neg(t, col):
+            nc.vector.tensor_scalar(out=negm[t][:, col:col + 1], in0=mrow[t][:, col:col + 1], scalar1=-1.0,
+                                    scalar2=None, op0=ALU.mult)
 
-        for n in range(NPAIR + 1):
-            k, j = divmod(n, HT)
-            if j == 0 and k + 3 < NCH:
-                load_mem(k + 3)
-            if n + 1 < NPAIR:
-                product(n + 1, 1)
-            if n < NPAIR:
-                a1(n)
-                v1(n)
-            if n >= 1:
-                a2(n - 1)
-                v2(n - 1)
-            if n + 1 < NPAIR:
-                product(n + 1, 0)
-            ka, ba = divmod(n + LEAD, HT)
-            if ka + 2 < NCH:
-                mem_transposes(ka + 2, ba)
-            if k + 2 < NCH:
-                if j == 0:
-                    mem_tiles(k + 2)
-                mem_evac(k + 2, j)
-            if k + 1 < NCH:
-                if j == 0:
-                    mem_square_vec(k + 1)
-                elif j == 1:
-                    quant(k + 1, "msq")
-                elif j == 2:
-                    quant(k + 1, "mgrp")
-            if j == 3:
-                max0(k)
-
-        negm = [const.tile([P, 1], F32, name="negm%d" % t) for t in range(HT)]
-        mrow = [const.tile([P, 1], F32, name="mrow%d" % t) for t in range(HT)]
-        sums = [const.tile([P, 1], F32, name="sums%d" % t) for t in range(HT)]
-        rs = [const.tile([P, 1], F32, name="rs%d" % t) for t in range(HT)]
-
-        def row_max(t):
-            nc.vector.tensor_reduce(out=mrow[t][:], in_=(mxp[:] if t == 0 else s_all[t][:]), axis=AX.X, op=ALU.max)
-            nc.vector.tensor_scalar(out=negm[t][:], in0=mrow[t][:], scalar1=-1.0, scalar2=None, op0=ALU.mult)
-
-        def row_exp(t):
-            nc.scalar.activation(out=s_all[t][:], in_=s_all[t][:], func=AF.Exp,
-                                 bias=negm[t][:], scale=1.0, accum_out=sums[t][:])
+        def row_exp(t, c0, cn, col, total):
+            nc.scalar.activation(out=s_all[t][:, c0:c0 + cn], in_=s_all[t][:, c0:c0 + cn], func=AF.Exp,
+                                 bias=negm[t][:, col:col + 1], scale=1.0, accum_out=total[:])
 
         def row_recip(t):
             nc.vector.reciprocal(out=rs[t][:], in_=sums[t][:])
 
-        def row_scale_store(t, q, eng):
-            cs = slice(q * 1024, (q + 1) * 1024)
-            piece = s_all[t][:, cs]
+        def row_scale_store(t, c0, cn, eng, by):
+            cols = s_all[t][:, c0:c0 + cn]
             if eng == "v":
-                nc.vector.tensor_scalar(out=piece, in0=piece, scalar1=rs[t][:], scalar2=None, op0=ALU.mult)
+                nc.vector.tensor_scalar(out=cols, in0=cols, scalar1=by[:], scalar2=None, op0=ALU.mult)
             elif eng == "a":
-                nc.scalar.activation(out=piece, in_=piece, func=AF.Copy, scale=rs[t][:])
+                nc.scalar.activation(out=cols, in_=cols, func=AF.Copy, scale=by[:])
             else:
-                nc.gpsimd.tensor_scalar(out=piece, in0=piece, scalar1=rs[t][:], scalar2=0.0,
-                                        op0=ALU.mult, op1=ALU.add)
-            nc.sync.dma_start(out=out2d[t * P:(t + 1) * P, cs], in_=piece)
+                nc.gpsimd.tensor_scalar(out=cols, in0=cols, scalar1=by[:], scalar2=0.0, op0=ALU.mult, op1=ALU.add)
+            nc.sync.dma_start(out=out2d[t * P:(t + 1) * P, c0:c0 + cn], in_=cols)
 
-        row_max(0)
-        row_exp(0)
-        row_max(1)
+        for i in range(HT * NQ):
+            root_recip(i)
+            recip_square(i)
+
         for t in range(HT):
-            if t + 1 < HT:
-                row_exp(t + 1)
-            row_recip(t)
-            last = t == HT - 1
-            row_scale_store(t, 0, "v")
-            row_scale_store(t, 1, "v" if last else "g")
-            row_scale_store(t, 2, "a" if last else "g")
-            row_scale_store(t, 3, "g")
-            if t + 2 < HT:
-                row_max(t + 2)
+            for q in range(NQ):
+                score(t, 2 * q)
+                if q == 1 and t >= 1:
+                    row_neg(t - 1, 0)
+                    if t == 2:
+                        row_recip(0)
+                        for c in range(NQ):
+                            row_scale_store(0, c * PIECE, PIECE, "a", rs[0])
+                    row_exp(t - 1, 0, C, 0, sums[t - 1])
+                if q:
+                    part_max(t, q - 1)
+                score(t, 2 * q + 1)
+                if q == NQ - 1:
+                    part_max(t, q)
+                if q == 0 and t >= 1:
+                    row_max(t - 1, 0, NQ)
+                if t == last and q == 2:
+                    row_max(t, 0, 2)
+                if (t, q) == RECIP[1]:
+                    row_recip(1)
+                    for c in range(NQ):
+                        row_scale_store(1, c * PIECE, PIECE, "g", rs[1])
+                if (t, q) == RECIP[2]:
+                    row_recip(2)
+                    row_neg(t, 0)
+                    row_exp(t, 0, HALF, 0, sums_a)
+        row_max(last, 1, NQ)
+        row_neg(last, 1)
+        for c in range(NQ):
+            row_scale_store(2, c * PIECE, PIECE, ENG2[c], rs[2])
+        nc.scalar.activation(out=fold[:], in_=mrow[last][:, 0:1], func=AF.Exp, bias=negm[last][:, 1:2], scale=1.0)
+        row_exp(last, HALF, HALF, 1, sums[last])
+        nc.vector.scalar_tensor_tensor(out=sums[last][:], in0=sums_a[:], scalar=fold[:], in1=sums[last][:],
+                                       op0=ALU.mult, op1=ALU.add)
+        row_recip(last)
+        row_scale_store(last, HALF, 512, "v", rs[last])
+        nc.vector.tensor_tensor(out=rs_a[:], in0=rs[last][:], in1=fold[:], op=ALU.mult)
+        row_scale_store(last, HALF + 512, 512, "v", rs[last])
+        row_scale_store(last, HALF + 1024, 1024, "v", rs[last])
+        row_scale_store(last, 0, 1024, "v", rs_a)
+        row_scale_store(last, 1024, 1024, "v", rs_a)

@@ -21,20 +21,23 @@ G = W // 512
 PIECE = 1024
 NQ = C // PIECE
 S_SQ = (0, 1)
-RECIP = (None, (3, 0), (3, 2))
+RECIP = (None, (3, 1), (3, 2))
 ENG1 = "ggvv"
 NAT_BUFS = 2
-S_FROM = 0
 DEFER = 5
-S_CELLS = 0
-S_KEVAC = (1, 2, 3)
+S_CHUNKS = ()
+S_CELLS = 128
+POS = 0
+EV_FIRST = 2
+V_EVACS = ()
+KEY_STEPS = {1: 1, 3: 2, 5: 3}
 ENG2 = "ggvv"
 EPS = 1e-8
 FLOPS = 2 * 2 * H * C * W
 
 
 def s_cells(k):
-    return S_CELLS if k >= S_FROM else 0
+    return S_CELLS if k in S_CHUNKS else 0
 
 
 def tile_contentaddressing_t_kernel(tc, memory, keys, betas, mask, out):
@@ -49,6 +52,7 @@ def tile_contentaddressing_t_kernel(tc, memory, keys, betas, mask, out):
         natp = ctx.enter_context(tc.tile_pool(name="natp", bufs=NAT_BUFS))
         grp = ctx.enter_context(tc.tile_pool(name="grp", bufs=2))
         memp = ctx.enter_context(tc.tile_pool(name="memp", bufs=NCH - DEFER))
+        head = ctx.enter_context(tc.tile_pool(name="head", bufs=2))
         cod = ctx.enter_context(tc.tile_pool(name="cod", bufs=3))
         psum = ctx.enter_context(tc.psum_pool(name="psum", bufs=4))
         ctx.enter_context(tc.manual_schedule())
@@ -81,12 +85,11 @@ def tile_contentaddressing_t_kernel(tc, memory, keys, betas, mask, out):
             nat[k] = t_nat
 
         nc.scalar.dma_start(out=brow[0:HT, :], in_=betas.rearrange("o (t p) -> (o t) p", p=P))
-        for t in range(2):
+        for t in range(HT):
             load_head(mask_nat, mask2d, t)
+        for t in range(2):
             load_head(keys_nat, keys2d, t)
         load_mem(0)
-        for t in range(2, HT):
-            load_head(mask_nat, mask2d, t)
         load_mem(1)
         for t in range(2, HT):
             load_head(keys_nat, keys2d, t)
@@ -94,10 +97,9 @@ def tile_contentaddressing_t_kernel(tc, memory, keys, betas, mask, out):
         beta_f = const.tile([P, HT], F32, name="beta_f")
         kn2 = const.tile([P, HT], F32, name="kn2")
         kn = const.tile([P, HT], F32, name="kn")
-        junk = const.tile([P, P], F32, name="junk")
+        junk = const.tile([P, W], BF16, name="junk")
         kcodes = const.tile([P, HT * 512], U32, name="kcodes", align_bytes=64)
         kscale = const.tile([P, HT * 512], U8, name="kscale", align_bytes=64)
-        mask_grp = [const.tile([P, G, P, 4], BF16, name="mask_grp%d" % t, align_bytes=64) for t in range(HT)]
         s_all = [const.tile([P, C], F32, name="s%d" % t) for t in range(HT)]
         mem_codes = [const.tile([P, G * CHUNK], U32, name="mem_codes%d" % k, align_bytes=64) for k in range(NCH)]
         mem_scale = [const.tile([P, G * CHUNK], U8, name="mem_scale%d" % k, align_bytes=64) for k in range(NCH)]
@@ -111,59 +113,42 @@ def tile_contentaddressing_t_kernel(tc, memory, keys, betas, mask, out):
 
         flat = "p g h s -> p (g h s)"
 
-        def head_transposes(t, src):
-            words = (mask_nat if src == 1 else keys_nat)[t][:].bitcast(F32)
+        def mask_square(t):
+            m2 = head.tile([P, W], BF16, name="m2", bufs=HT)
+            m = mask_nat[t][:]
+            nc.vector.tensor_tensor(out=m2[:], in0=m, in1=m, op=ALU.mult)
+            mp[("h", t, 1)] = m2
+
+        def key_mask(t):
+            km = head.tile([P, W], F32, name="km")
+            nc.vector.tensor_tensor(out=km[:], in0=keys_nat[t][:], in1=mask_nat[t][:], op=ALU.mult)
+            mp[("km", t)] = km
+
+        def key_mask2(t):
+            km2 = head.tile([P, W], BF16, name="km2")
+            nc.vector.tensor_tensor(out=km2[:], in0=mp[("km", t)][:], in1=mask_nat[t][:], op=ALU.mult)
+            mp[("h", t, 0)] = km2
+
+        def key_norm2(t):
+            nc.scalar.activation(out=junk[:], in_=mp[("km", t)][:], func=AF.Square, accum_out=kn2[:, t:t + 1])
+
+        def head_transposes(t, op):
+            words = mp[("h", t, op)][:].bitcast(F32)
             xt = acc_bank([P, 2 * G, P])
             for i in range(2 * G):
                 nc.tensor.transpose(out=xt[:, i, :], in_=words[:, i * P:(i + 1) * P], identity=ident_f[:])
-            mp[("x", t, src)] = xt
+            mp[("x", t, op)] = xt
 
-        def mask_prep(t):
-            xt = mp[("x", t, 1)]
-            nc.scalar.copy(out=mask_grp[t][:].bitcast(F32), in_=xt[:].rearrange("p (g u) h -> p g h u", u=2))
-            m2 = grp.tile([P, G, P, 4], BF16, name="m2_grp", bufs=HT, align_bytes=64)
-            for g in range(G):
-                nc.scalar.activation(
-                    out=m2[:, g].rearrange("p h (u e) -> p h u e", e=2),
-                    in_=xt[:, 2 * g:2 * g + 2, :].bitcast(BF16).rearrange("p u (h e) -> p h u e", e=2),
-                    func=AF.Square)
-            mp[("q", t, 1)] = m2
-
-        def key_evac(t):
-            xt = mp[("x", t, 0)]
-            kg = grp.tile([P, G, P, 4], BF16, name="keys_grp", align_bytes=64)
-            copy = nc.scalar.copy if t in S_KEVAC else nc.vector.tensor_copy
-            copy(out=kg[:].bitcast(F32), in_=xt[:].rearrange("p (g u) h -> p g h u", u=2))
-            mp[("kg", t)] = kg
-
-        def key_prep(t):
-            kg = mp[("kg", t)]
-            km = grp.tile([P, G, P, 4], F32, name="km")
-            nc.vector.tensor_tensor(out=km[:].rearrange(flat), in0=kg[:].rearrange(flat),
-                                    in1=mask_grp[t][:].rearrange(flat), op=ALU.mult)
-            mp[("km", t)] = km
-
-        def key_square(t):
-            km2 = grp.tile([P, G, P, 4], BF16, name="km2_grp", align_bytes=64)
-            nc.vector.tensor_tensor(out=km2[:].rearrange(flat), in0=mp[("km", t)][:].rearrange(flat),
-                                    in1=mask_grp[t][:].rearrange(flat), op=ALU.mult)
-            mp[("q", t, 0)] = km2
+        def head_evac(t, op):
+            hg = head.tile([P, G, P, 4], BF16, name="hgrp", bufs=HT, align_bytes=64)
+            copy = nc.vector.tensor_copy if (t, op) in V_EVACS else nc.scalar.copy
+            copy(out=hg[:].bitcast(F32), in_=mp[("x", t, op)][:].rearrange("p (g u) h -> p g h u", u=2))
+            mp[("q", t, op)] = hg
 
         def head_quant(t, op):
             cs = slice(t * 512 + op * 256, t * 512 + op * 256 + 256)
             nc.vector.quantize_mx(out=kcodes[:, cs].bitcast(FP8X4), scales=kscale[:, cs],
                                   in_=mp[("q", t, op)][:].rearrange(flat))
-
-        def key_gram(t):
-            gram = acc_bank([P, P])
-            for i in range(4 * G):
-                col = mp[("km", t)][:, i // 4, :, i % 4]
-                nc.tensor.matmul(out=gram[:], lhsT=col, rhs=col, start=(i == 0), stop=(i == 4 * G - 1))
-            mp[("gram", t)] = gram
-
-        def key_norm2(t):
-            nc.vector.scalar_tensor_tensor(out=junk[:], in0=mp[("gram", t)][:], scalar=1.0, in1=ident_f[:],
-                                           op0=ALU.mult, op1=ALU.mult, accum_out=kn2[:, t:t + 1])
 
         def mem_transposes(k, b):
             g, half = divmod(b, 2)
@@ -228,75 +213,71 @@ def tile_contentaddressing_t_kernel(tc, memory, keys, betas, mask, out):
 
         BANKS = (0, 2, 1, 3)
 
-        for t in range(2):
+        for t in range(HT):
+            mask_square(t)
             head_transposes(t, 1)
-            head_transposes(t, 0)
-        for b in BANKS:
-            mem_transposes(0, b)
-        mask_prep(0)
-        key_evac(0)
-        key_prep(0)
-        key_evac(1)
-        mask_prep(1)
-        head_transposes(2, 1)
-        bT = acc_bank([P, P])
+            head_evac(t, 1)
+        bT = t_bank([P, P], F32)
         nc.tensor.transpose(out=bT[:].bitcast(BF16)[:, 0:P], in_=brow[:], identity=ident_b[:])
+        for b in BANKS[0:3]:
+            mem_transposes(0, b)
+        nc.vector.tensor_copy(out=beta_f[:], in_=bT[:].bitcast(BF16)[:, 0:HT])
+        mem_transposes(0, BANKS[3])
+        key_mask(0)
+        key_mask(1)
         for b in BANKS:
             mem_evac(0, b)
-        head_transposes(3, 1)
-        key_prep(1)
-        nc.vector.tensor_copy(out=beta_f[:], in_=bT[:].bitcast(BF16)[:, 0:HT])
-        for b in BANKS:
-            mem_transposes(1, b)
-        key_square(0)
-        head_quant(0, 1)
-        head_quant(1, 1)
-        mask_prep(2)
-        mask_prep(3)
+        key_mask2(0)
+        for t in range(HT):
+            head_quant(t, 1)
         mem_square(0)
         sq_quant(0)
-        head_quant(2, 1)
-        head_quant(3, 1)
-        mem_quant(0)
+        for b in BANKS:
+            mem_transposes(1, b)
         for b in BANKS:
             mem_evac(1, b)
-        key_square(1)
+        head_transposes(0, 0)
+        head_evac(0, 0)
+        key_norm2(0)
+        mem_quant(0)
+        key_mask2(1)
 
         for k in range(NCH):
             if k + 2 < NCH:
                 load_mem(k + 2)
-            if k in (0, 1):
-                head_transposes(k + 2, 0)
+            if k >= EV_FIRST and k + 2 < NCH:
+                for b in BANKS:
+                    mem_transposes(k + 2, b)
+                for b in BANKS:
+                    mem_evac(k + 2, b)
+            if k in KEY_STEPS:
+                t = KEY_STEPS[k]
+                head_transposes(t, 0)
             for t in range(HT):
                 mp[("mn2", t, k)] = product(t, k, 1, acc_bank([P, CHUNK]))
                 norm_root(t, k)
+            if k in KEY_STEPS:
+                t = KEY_STEPS[k]
+                head_evac(t, 0)
+                key_norm2(t)
             if k + 1 < NCH:
                 mem_square(k + 1)
                 sq_quant(k + 1)
                 if k + 1 < DEFER:
                     mem_quant(k + 1)
-            if k + 2 < NCH:
+            if k in KEY_STEPS and KEY_STEPS[k] + 1 < HT:
+                key_mask(KEY_STEPS[k] + 1)
+                key_mask2(KEY_STEPS[k] + 1)
+            if k < EV_FIRST and k + 2 < NCH:
                 for b in BANKS:
                     mem_transposes(k + 2, b)
                 for b in BANKS:
                     mem_evac(k + 2, b)
-            if k in (0, 1, 2, 3):
-                key_gram(k)
-            if k == 2:
-                head_quant(0, 0)
-                head_quant(1, 0)
-            if k in (0, 1):
-                key_evac(k + 2)
-            if k in (1, 2):
-                key_prep(k + 1)
-            if k in (0, 1, 2, 3):
-                key_norm2(k)
         nc.scalar.activation(out=kn[:], in_=kn2[:], func=AF.Sqrt, bias=b_tiny[:], scale=1.0)
+        for t in range(HT):
+            head_quant(t, 0)
         for k in range(DEFER, NCH):
             mem_quant(k)
-        for t in (2, 3):
-            key_square(t)
-            head_quant(t, 0)
 
         HALF = C // 2
         last = HT - 1
@@ -319,10 +300,11 @@ def tile_contentaddressing_t_kernel(tc, memory, keys, betas, mask, out):
 
         def recip_square(i):
             t, q = divmod(i, NQ)
+            a, b = piece(t, q)[:, 0:CHUNK], piece(t, q)
             if i in S_SQ:
-                nc.scalar.activation(out=piece(t, q), in_=piece(t, q), func=AF.Square)
-            else:
-                nc.gpsimd.tensor_tensor(out=piece(t, q), in0=piece(t, q), in1=piece(t, q), op=ALU.mult)
+                nc.scalar.activation(out=a, in_=a, func=AF.Square)
+                b = b[:, CHUNK:]
+            nc.gpsimd.tensor_tensor(out=b, in0=b, in1=b, op=ALU.mult)
 
         def score(t, k):
             bank = acc_bank([P, CHUNK]) if k % 2 == 0 else t_bank([P, CHUNK], F32)
@@ -358,6 +340,12 @@ def tile_contentaddressing_t_kernel(tc, memory, keys, betas, mask, out):
                 nc.gpsimd.tensor_scalar(out=cols, in0=cols, scalar1=by[:], scalar2=0.0, op0=ALU.mult, op1=ALU.add)
             nc.sync.dma_start(out=out2d[t * P:(t + 1) * P, c0:c0 + cn], in_=cols)
 
+        def recip0():
+            row_recip(0)
+            for c in range(NQ):
+                row_scale_store(0, c * PIECE, PIECE, "a", rs[0])
+            row_exp(1, 0, C, 0, sums[1])
+
         for i in range(HT * NQ):
             root_recip(i)
             recip_square(i)
@@ -367,14 +355,15 @@ def tile_contentaddressing_t_kernel(tc, memory, keys, betas, mask, out):
                 score(t, 2 * q)
                 if q == 1 and t >= 1:
                     row_neg(t - 1, 0)
-                    if t == 2:
-                        row_recip(0)
-                        for c in range(NQ):
-                            row_scale_store(0, c * PIECE, PIECE, "a", rs[0])
-                    row_exp(t - 1, 0, C, 0, sums[t - 1])
+                    if t != 2:
+                        row_exp(t - 1, 0, C, 0, sums[t - 1])
                 if q:
                     part_max(t, q - 1)
+                if q == 1 and t == 2 and POS == 0:
+                    recip0()
                 score(t, 2 * q + 1)
+                if q == 1 and t == 2 and POS == 1:
+                    recip0()
                 if q == NQ - 1:
                     part_max(t, q)
                 if q == 0 and t >= 1:

@@ -24,12 +24,18 @@ S_SQ = (0, 1)
 RECIP = (None, (3, 1), (3, 2))
 ENG1 = "ggvv"
 NAT_BUFS = 2
-DEFER = 5
+DEFER = 4
 S_CHUNKS = ()
 S_CELLS = 128
+ENG0 = "aaaa"
 POS = 0
 EV_FIRST = 2
 V_EVACS = ()
+SQ_BUFS = 1
+MEM_BUFS = 4
+LAG = 1
+V_NORM = ()
+NORM_AT = {0: -1, 1: -1, 2: 3, 3: 5}
 KEY_STEPS = {1: 1, 3: 2, 5: 3}
 ENG2 = "ggvv"
 EPS = 1e-8
@@ -51,7 +57,7 @@ def tile_contentaddressing_t_kernel(tc, memory, keys, betas, mask, out):
         const = ctx.enter_context(tc.tile_pool(name="const", bufs=1))
         natp = ctx.enter_context(tc.tile_pool(name="natp", bufs=NAT_BUFS))
         grp = ctx.enter_context(tc.tile_pool(name="grp", bufs=2))
-        memp = ctx.enter_context(tc.tile_pool(name="memp", bufs=NCH - DEFER))
+        memp = ctx.enter_context(tc.tile_pool(name="memp", bufs=MEM_BUFS))
         head = ctx.enter_context(tc.tile_pool(name="head", bufs=2))
         cod = ctx.enter_context(tc.tile_pool(name="cod", bufs=3))
         psum = ctx.enter_context(tc.psum_pool(name="psum", bufs=4))
@@ -130,7 +136,12 @@ def tile_contentaddressing_t_kernel(tc, memory, keys, betas, mask, out):
             mp[("h", t, 0)] = km2
 
         def key_norm2(t):
-            nc.scalar.activation(out=junk[:], in_=mp[("km", t)][:], func=AF.Square, accum_out=kn2[:, t:t + 1])
+            km = mp[("km", t)][:]
+            if t in V_NORM:
+                nc.vector.scalar_tensor_tensor(out=junk[:], in0=km, scalar=1.0, in1=km, op0=ALU.mult, op1=ALU.mult,
+                                               accum_out=kn2[:, t:t + 1])
+            else:
+                nc.scalar.activation(out=junk[:], in_=km, func=AF.Square, accum_out=kn2[:, t:t + 1])
 
         def head_transposes(t, op):
             words = mp[("h", t, op)][:].bitcast(F32)
@@ -167,7 +178,7 @@ def tile_contentaddressing_t_kernel(tc, memory, keys, betas, mask, out):
             g, half = divmod(b, 2)
             if b == BANKS[0]:
                 mp[(k, "mem")] = memp.tile([P, G, CHUNK, 4], BF16, name="mem_grp", align_bytes=64)
-                mp[(k, "sq")] = grp.tile([P, G, CHUNK, 4], BF16, name="sq_grp", align_bytes=64)
+                mp[(k, "sq")] = grp.tile([P, G, CHUNK, 4], BF16, name="sq_grp", bufs=SQ_BUFS, align_bytes=64)
             nc.scalar.copy(out=mp[(k, "mem")][:].bitcast(F32)[:, g, 256 * half:256 * half + 256, :],
                            in_=mp[(k, "tb", b)][:].rearrange("p u r -> p r u"))
             n = s_cells(k)
@@ -221,7 +232,7 @@ def tile_contentaddressing_t_kernel(tc, memory, keys, betas, mask, out):
         nc.tensor.transpose(out=bT[:].bitcast(BF16)[:, 0:P], in_=brow[:], identity=ident_b[:])
         for b in BANKS[0:3]:
             mem_transposes(0, b)
-        nc.vector.tensor_copy(out=beta_f[:], in_=bT[:].bitcast(BF16)[:, 0:HT])
+        nc.vector.tensor_scalar(out=beta_f[:], in0=bT[:].bitcast(BF16)[:, 0:HT], scalar1=-1.0, scalar2=None, op0=ALU.mult)
         mem_transposes(0, BANKS[3])
         key_mask(0)
         key_mask(1)
@@ -238,9 +249,9 @@ def tile_contentaddressing_t_kernel(tc, memory, keys, betas, mask, out):
             mem_evac(1, b)
         head_transposes(0, 0)
         head_evac(0, 0)
-        key_norm2(0)
-        mem_quant(0)
-        key_mask2(1)
+        for t in range(HT):
+            if NORM_AT[t] == -1:
+                key_norm2(t)
 
         for k in range(NCH):
             if k + 2 < NCH:
@@ -259,12 +270,19 @@ def tile_contentaddressing_t_kernel(tc, memory, keys, betas, mask, out):
             if k in KEY_STEPS:
                 t = KEY_STEPS[k]
                 head_evac(t, 0)
-                key_norm2(t)
+            for t in range(HT):
+                if NORM_AT[t] == k and t not in V_NORM:
+                    key_norm2(t)
             if k + 1 < NCH:
                 mem_square(k + 1)
                 sq_quant(k + 1)
-                if k + 1 < DEFER:
-                    mem_quant(k + 1)
+            if k + 1 - LAG < DEFER:
+                mem_quant(k + 1 - LAG)
+            if k == 0:
+                key_mask2(1)
+            for t in range(HT):
+                if NORM_AT[t] == k and t in V_NORM:
+                    key_norm2(t)
             if k in KEY_STEPS and KEY_STEPS[k] + 1 < HT:
                 key_mask(KEY_STEPS[k] + 1)
                 key_mask2(KEY_STEPS[k] + 1)
@@ -282,7 +300,6 @@ def tile_contentaddressing_t_kernel(tc, memory, keys, betas, mask, out):
         HALF = C // 2
         last = HT - 1
         pmx = [const.tile([P, NQ], F32, name="pmx%d" % t) for t in range(HT)]
-        negm = [const.tile([P, 2], F32, name="negm%d" % t) for t in range(HT)]
         mrow = [const.tile([P, 2], F32, name="mrow%d" % t) for t in range(HT)]
         sums = [const.tile([P, 1], F32, name="sums%d" % t) for t in range(HT)]
         sums_a = const.tile([P, 1], F32, name="sums_a")
@@ -314,18 +331,14 @@ def tile_contentaddressing_t_kernel(tc, memory, keys, betas, mask, out):
                                            op0=ALU.mult, op1=ALU.mult)
 
         def part_max(t, q):
-            nc.vector.tensor_reduce(out=pmx[t][:, q:q + 1], in_=piece(t, q), axis=AX.X, op=ALU.max)
+            nc.vector.tensor_reduce(out=pmx[t][:, q:q + 1], in_=piece(t, q), axis=AX.X, op=ALU.min)
 
         def row_max(t, col, nq):
-            nc.vector.tensor_reduce(out=mrow[t][:, col:col + 1], in_=pmx[t][:, 0:nq], axis=AX.X, op=ALU.max)
-
-        def row_neg(t, col):
-            nc.vector.tensor_scalar(out=negm[t][:, col:col + 1], in0=mrow[t][:, col:col + 1], scalar1=-1.0,
-                                    scalar2=None, op0=ALU.mult)
+            nc.vector.tensor_reduce(out=mrow[t][:, col:col + 1], in_=pmx[t][:, 0:nq], axis=AX.X, op=ALU.min)
 
         def row_exp(t, c0, cn, col, total):
             nc.scalar.activation(out=s_all[t][:, c0:c0 + cn], in_=s_all[t][:, c0:c0 + cn], func=AF.Exp,
-                                 bias=negm[t][:, col:col + 1], scale=1.0, accum_out=total[:])
+                                 bias=mrow[t][:, col:col + 1], scale=-1.0, accum_out=total[:])
 
         def row_recip(t):
             nc.vector.reciprocal(out=rs[t][:], in_=sums[t][:])
@@ -343,7 +356,7 @@ def tile_contentaddressing_t_kernel(tc, memory, keys, betas, mask, out):
         def recip0():
             row_recip(0)
             for c in range(NQ):
-                row_scale_store(0, c * PIECE, PIECE, "a", rs[0])
+                row_scale_store(0, c * PIECE, PIECE, ENG0[c], rs[0])
             row_exp(1, 0, C, 0, sums[1])
 
         for i in range(HT * NQ):
@@ -353,10 +366,6 @@ def tile_contentaddressing_t_kernel(tc, memory, keys, betas, mask, out):
         for t in range(HT):
             for q in range(NQ):
                 score(t, 2 * q)
-                if q == 1 and t >= 1:
-                    row_neg(t - 1, 0)
-                    if t != 2:
-                        row_exp(t - 1, 0, C, 0, sums[t - 1])
                 if q:
                     part_max(t, q - 1)
                 if q == 1 and t == 2 and POS == 0:
@@ -368,6 +377,8 @@ def tile_contentaddressing_t_kernel(tc, memory, keys, betas, mask, out):
                     part_max(t, q)
                 if q == 0 and t >= 1:
                     row_max(t - 1, 0, NQ)
+                    if t != 2:
+                        row_exp(t - 1, 0, C, 0, sums[t - 1])
                 if t == last and q == 2:
                     row_max(t, 0, 2)
                 if (t, q) == RECIP[1]:
@@ -376,13 +387,11 @@ def tile_contentaddressing_t_kernel(tc, memory, keys, betas, mask, out):
                         row_scale_store(1, c * PIECE, PIECE, "g", rs[1])
                 if (t, q) == RECIP[2]:
                     row_recip(2)
-                    row_neg(t, 0)
                     row_exp(t, 0, HALF, 0, sums_a)
         row_max(last, 1, NQ)
-        row_neg(last, 1)
         for c in range(NQ):
             row_scale_store(2, c * PIECE, PIECE, ENG2[c], rs[2])
-        nc.scalar.activation(out=fold[:], in_=mrow[last][:, 0:1], func=AF.Exp, bias=negm[last][:, 1:2], scale=1.0)
+        nc.scalar.activation(out=fold[:], in_=mrow[last][:, 0:1], func=AF.Exp, bias=mrow[last][:, 1:2], scale=-1.0)
         row_exp(last, HALF, HALF, 1, sums[last])
         nc.vector.scalar_tensor_tensor(out=sums[last][:], in0=sums_a[:], scalar=fold[:], in1=sums[last][:],
                                        op0=ALU.mult, op1=ALU.add)

@@ -20,21 +20,24 @@ NCH = C // CHUNK
 G = W // 512
 PIECE = 1024
 NQ = C // PIECE
-S_SQ = (0, 1)
+S_SQ = (0, 1, 3)
 RECIP = (None, (3, 1), (3, 2))
-ENG1 = "ggvv"
+ENG1 = "vggg"
 NAT_BUFS = 2
 DEFER = 4
 S_CHUNKS = ()
 S_CELLS = 128
 ENG0 = "aaaa"
-POS = 0
-EV_FIRST = 2
+HQ = 2
+COD = 2
+A1 = 4
+STEP = 2
+FIRST = True
 V_EVACS = ()
 SQ_BUFS = 1
 MEM_BUFS = 4
 LAG = 1
-V_NORM = ()
+LATE = (2, 3)
 NORM_AT = {0: -1, 1: -1, 2: 3, 3: 5}
 KEY_STEPS = {1: 1, 3: 2, 5: 3}
 ENG2 = "ggvv"
@@ -59,7 +62,7 @@ def tile_contentaddressing_t_kernel(tc, memory, keys, betas, mask, out):
         grp = ctx.enter_context(tc.tile_pool(name="grp", bufs=2))
         memp = ctx.enter_context(tc.tile_pool(name="memp", bufs=MEM_BUFS))
         head = ctx.enter_context(tc.tile_pool(name="head", bufs=2))
-        cod = ctx.enter_context(tc.tile_pool(name="cod", bufs=3))
+        cod = ctx.enter_context(tc.tile_pool(name="cod", bufs=COD))
         psum = ctx.enter_context(tc.psum_pool(name="psum", bufs=4))
         ctx.enter_context(tc.manual_schedule())
 
@@ -109,6 +112,7 @@ def tile_contentaddressing_t_kernel(tc, memory, keys, betas, mask, out):
         s_all = [const.tile([P, C], F32, name="s%d" % t) for t in range(HT)]
         mem_codes = [const.tile([P, G * CHUNK], U32, name="mem_codes%d" % k, align_bytes=64) for k in range(NCH)]
         mem_scale = [const.tile([P, G * CHUNK], U8, name="mem_scale%d" % k, align_bytes=64) for k in range(NCH)]
+        hgrp = [const.tile([P, HT, G, P, 4], BF16, name="hgrp%d" % op, align_bytes=64) for op in range(2)]
         mp = {}
 
         def t_bank(shape, dtype):
@@ -137,7 +141,7 @@ def tile_contentaddressing_t_kernel(tc, memory, keys, betas, mask, out):
 
         def key_norm2(t):
             km = mp[("km", t)][:]
-            if t in V_NORM:
+            if t in LATE:
                 nc.vector.scalar_tensor_tensor(out=junk[:], in0=km, scalar=1.0, in1=km, op0=ALU.mult, op1=ALU.mult,
                                                accum_out=kn2[:, t:t + 1])
             else:
@@ -151,15 +155,13 @@ def tile_contentaddressing_t_kernel(tc, memory, keys, betas, mask, out):
             mp[("x", t, op)] = xt
 
         def head_evac(t, op):
-            hg = head.tile([P, G, P, 4], BF16, name="hgrp", bufs=HT, align_bytes=64)
             copy = nc.vector.tensor_copy if (t, op) in V_EVACS else nc.scalar.copy
-            copy(out=hg[:].bitcast(F32), in_=mp[("x", t, op)][:].rearrange("p (g u) h -> p g h u", u=2))
-            mp[("q", t, op)] = hg
+            copy(out=hgrp[op][:, t].bitcast(F32), in_=mp[("x", t, op)][:].rearrange("p (g u) h -> p g h u", u=2))
 
-        def head_quant(t, op):
-            cs = slice(t * 512 + op * 256, t * 512 + op * 256 + 256)
+        def head_quant(t, n, op):
+            cs = slice(op * HT * 256 + t * 256, op * HT * 256 + (t + n) * 256)
             nc.vector.quantize_mx(out=kcodes[:, cs].bitcast(FP8X4), scales=kscale[:, cs],
-                                  in_=mp[("q", t, op)][:].rearrange(flat))
+                                  in_=hgrp[op][:, t:t + n].rearrange("p t g h s -> p (t g h s)"))
 
         def mem_transposes(k, b):
             g, half = divmod(b, 2)
@@ -189,8 +191,11 @@ def tile_contentaddressing_t_kernel(tc, memory, keys, betas, mask, out):
                     func=AF.Square)
 
         def mem_square(k):
-            m = mp[(k, "mem")][:].rearrange(flat)[:, 4 * s_cells(k):]
-            nc.vector.tensor_tensor(out=mp[(k, "sq")][:].rearrange(flat)[:, 4 * s_cells(k):], in0=m, in1=m, op=ALU.mult)
+            for g in range(G):
+                c0 = s_cells(k) if g == 0 else 0
+                m = mp[(k, "mem")][:, g, c0:, :].rearrange("p c s -> p (c s)")
+                nc.vector.tensor_tensor(out=mp[(k, "sq")][:, g, c0:, :].rearrange("p c s -> p (c s)"),
+                                        in0=m, in1=m, op=ALU.mult)
 
         def mem_quant(k):
             nc.vector.quantize_mx(out=mem_codes[k][:].bitcast(FP8X4), scales=mem_scale[k][:],
@@ -199,13 +204,16 @@ def tile_contentaddressing_t_kernel(tc, memory, keys, betas, mask, out):
         def sq_quant(k):
             dat = cod.tile([P, G * CHUNK], U32, name="sq_codes", align_bytes=64)
             scl = cod.tile([P, G * CHUNK], U8, name="sq_scale", align_bytes=64)
-            nc.vector.quantize_mx(out=dat[:].bitcast(FP8X4), scales=scl[:], in_=mp[(k, "sq")][:].rearrange(flat))
+            for g in range(G):
+                gs = slice(g * CHUNK, (g + 1) * CHUNK)
+                nc.vector.quantize_mx(out=dat[:, gs].bitcast(FP8X4), scales=scl[:, gs],
+                                      in_=mp[(k, "sq")][:, g].rearrange("p c s -> p (c s)"))
             mp[(k, "sqq")] = (dat, scl)
 
         def product(t, k, op, acc):
             dat, scl = (mem_codes[k], mem_scale[k]) if op == 0 else mp[(k, "sqq")]
             for g in range(G):
-                c0 = t * 512 + op * 256 + g * P
+                c0 = op * HT * 256 + t * 256 + g * P
                 nc.tensor.matmul_mx(
                     out=acc[:],
                     lhsT=kcodes[:, c0:c0 + P].bitcast(FP8X4),
@@ -239,8 +247,8 @@ def tile_contentaddressing_t_kernel(tc, memory, keys, betas, mask, out):
         for b in BANKS:
             mem_evac(0, b)
         key_mask2(0)
-        for t in range(HT):
-            head_quant(t, 1)
+        for t in range(0, HT, HQ):
+            head_quant(t, HQ, 1)
         mem_square(0)
         sq_quant(0)
         for b in BANKS:
@@ -256,46 +264,48 @@ def tile_contentaddressing_t_kernel(tc, memory, keys, betas, mask, out):
         for k in range(NCH):
             if k + 2 < NCH:
                 load_mem(k + 2)
-            if k >= EV_FIRST and k + 2 < NCH:
-                for b in BANKS:
-                    mem_transposes(k + 2, b)
-                for b in BANKS:
-                    mem_evac(k + 2, b)
             if k in KEY_STEPS:
                 t = KEY_STEPS[k]
                 head_transposes(t, 0)
-            for t in range(HT):
-                mp[("mn2", t, k)] = product(t, k, 1, acc_bank([P, CHUNK]))
-                norm_root(t, k)
+            for h in range(0, HT, STEP):
+                if k + 2 < NCH and FIRST:
+                    for b in BANKS[h:h + STEP]:
+                        mem_transposes(k + 2, b)
+                    for b in BANKS[h:h + STEP]:
+                        mem_evac(k + 2, b)
+                for t in range(h, h + STEP):
+                    mp[("mn2", t, k)] = product(t, k, 1, acc_bank([P, CHUNK]))
+                    norm_root(t, k)
+                if k + 2 < NCH and not FIRST:
+                    for b in BANKS[h:h + STEP]:
+                        mem_transposes(k + 2, b)
+                    for b in BANKS[h:h + STEP]:
+                        mem_evac(k + 2, b)
             if k in KEY_STEPS:
                 t = KEY_STEPS[k]
                 head_evac(t, 0)
             for t in range(HT):
-                if NORM_AT[t] == k and t not in V_NORM:
+                if NORM_AT[t] == k and t not in LATE:
                     key_norm2(t)
             if k + 1 < NCH:
                 mem_square(k + 1)
                 sq_quant(k + 1)
+            t_next = KEY_STEPS[k] + 1 if k in KEY_STEPS else HT
+            if t_next < HT:
+                key_mask(t_next)
             if k + 1 - LAG < DEFER:
                 mem_quant(k + 1 - LAG)
             if k == 0:
                 key_mask2(1)
-            for t in range(HT):
-                if NORM_AT[t] == k and t in V_NORM:
-                    key_norm2(t)
-            if k in KEY_STEPS and KEY_STEPS[k] + 1 < HT:
-                key_mask(KEY_STEPS[k] + 1)
-                key_mask2(KEY_STEPS[k] + 1)
-            if k < EV_FIRST and k + 2 < NCH:
-                for b in BANKS:
-                    mem_transposes(k + 2, b)
-                for b in BANKS:
-                    mem_evac(k + 2, b)
-        nc.scalar.activation(out=kn[:], in_=kn2[:], func=AF.Sqrt, bias=b_tiny[:], scale=1.0)
-        for t in range(HT):
-            head_quant(t, 0)
+            if t_next < HT:
+                key_mask2(t_next)
+        early = HT - len(LATE)
+        nc.scalar.activation(out=kn[:, 0:early], in_=kn2[:, 0:early], func=AF.Sqrt, bias=b_tiny[:], scale=1.0)
+        head_quant(0, HT, 0)
         for k in range(DEFER, NCH):
             mem_quant(k)
+        for t in LATE:
+            key_norm2(t)
 
         HALF = C // 2
         last = HT - 1
@@ -305,22 +315,27 @@ def tile_contentaddressing_t_kernel(tc, memory, keys, betas, mask, out):
         sums_a = const.tile([P, 1], F32, name="sums_a")
         fold = const.tile([P, 1], F32, name="fold")
         rs = [const.tile([P, 1], F32, name="rs%d" % t) for t in range(HT)]
+        rk = {t: const.tile([P, 1], F32, name="rk%d" % t) for t in LATE}
         rs_a = const.tile([P, 1], F32, name="rs_a")
 
         def piece(t, q):
             return s_all[t][:, q * PIECE:(q + 1) * PIECE]
 
-        def root_recip(i):
-            t, q = divmod(i, NQ)
-            nc.scalar.activation(out=piece(t, q), in_=piece(t, q), func=AF.Abs_reciprocal_sqrt,
+        def root_recip(i, n):
+            t, c0 = divmod(i * CHUNK, C)
+            cols = s_all[t][:, c0:c0 + n * CHUNK]
+            nc.scalar.activation(out=cols, in_=cols, func=AF.Abs_reciprocal_sqrt,
                                  bias=b_eps[:], scale=kn[:, t:t + 1])
 
-        def recip_square(i):
+        def scalar_square(i):
             t, q = divmod(i, NQ)
-            a, b = piece(t, q)[:, 0:CHUNK], piece(t, q)
+            a = piece(t, q)[:, 0:CHUNK]
             if i in S_SQ:
                 nc.scalar.activation(out=a, in_=a, func=AF.Square)
-                b = b[:, CHUNK:]
+
+        def gpsimd_square(i):
+            t, q = divmod(i, NQ)
+            b = piece(t, q)[:, CHUNK if i in S_SQ else 0:]
             nc.gpsimd.tensor_tensor(out=b, in0=b, in1=b, op=ALU.mult)
 
         def score(t, k):
@@ -330,8 +345,8 @@ def tile_contentaddressing_t_kernel(tc, memory, keys, betas, mask, out):
             nc.vector.scalar_tensor_tensor(out=col, in0=bank[:], scalar=beta_f[:, t:t + 1], in1=col,
                                            op0=ALU.mult, op1=ALU.mult)
 
-        def part_max(t, q):
-            nc.vector.tensor_reduce(out=pmx[t][:, q:q + 1], in_=piece(t, q), axis=AX.X, op=ALU.min)
+        def part_max(t, i, c0, cn):
+            nc.vector.tensor_reduce(out=pmx[t][:, i:i + 1], in_=s_all[t][:, c0:c0 + cn], axis=AX.X, op=ALU.min)
 
         def row_max(t, col, nq):
             nc.vector.tensor_reduce(out=mrow[t][:, col:col + 1], in_=pmx[t][:, 0:nq], axis=AX.X, op=ALU.min)
@@ -359,35 +374,56 @@ def tile_contentaddressing_t_kernel(tc, memory, keys, betas, mask, out):
                 row_scale_store(0, c * PIECE, PIECE, ENG0[c], rs[0])
             row_exp(1, 0, C, 0, sums[1])
 
+        def late_root(t):
+            nc.scalar.activation(out=rk[t][:], in_=kn2[:, t:t + 1], func=AF.Abs_reciprocal_sqrt, bias=b_tiny[:], scale=1.0)
+
+        def late_norm(t):
+            nc.scalar.activation(out=kn[:, t:t + 1], in_=kn2[:, t:t + 1], func=AF.Copy, scale=rk[t][:])
+
         for i in range(HT * NQ):
-            root_recip(i)
-            recip_square(i)
+            if i < 2:
+                root_recip(2 * i, 1)
+                root_recip(2 * i + 1, 1)
+                scalar_square(i)
+            elif i % 2 == 0:
+                if i // NQ + 1 in LATE:
+                    (late_root if i % NQ == 0 else late_norm)(i // NQ + 1)
+                if i < A1:
+                    root_recip(2 * i, 2)
+                    root_recip(2 * i + 2, 2)
+                else:
+                    root_recip(2 * i, 4)
+                scalar_square(i)
+                scalar_square(i + 1)
+            gpsimd_square(i)
 
         for t in range(HT):
             for q in range(NQ):
                 score(t, 2 * q)
-                if q:
-                    part_max(t, q - 1)
-                if q == 1 and t == 2 and POS == 0:
-                    recip0()
-                score(t, 2 * q + 1)
-                if q == 1 and t == 2 and POS == 1:
-                    recip0()
-                if q == NQ - 1:
-                    part_max(t, q)
                 if q == 0 and t >= 1:
-                    row_max(t - 1, 0, NQ)
+                    part_max(t - 1, 1, HALF, HALF)
+                if q == 2:
+                    part_max(t, 0, 0, HALF)
+                if q == 3 and t == last:
+                    part_max(t, 1, HALF, PIECE)
+                score(t, 2 * q + 1)
+                if q == 0 and t >= 1:
+                    row_max(t - 1, 0, 2)
                     if t != 2:
                         row_exp(t - 1, 0, C, 0, sums[t - 1])
+                if q == 1 and t == 2:
+                    recip0()
                 if t == last and q == 2:
-                    row_max(t, 0, 2)
+                    row_max(t, 0, 1)
                 if (t, q) == RECIP[1]:
                     row_recip(1)
                     for c in range(NQ):
-                        row_scale_store(1, c * PIECE, PIECE, "g", rs[1])
+                        row_scale_store(1, c * PIECE, PIECE, ENG1[c], rs[1])
                 if (t, q) == RECIP[2]:
                     row_recip(2)
                     row_exp(t, 0, HALF, 0, sums_a)
+        part_max(last, 2, C - PIECE, CHUNK)
+        part_max(last, 3, C - CHUNK, CHUNK)
         row_max(last, 1, NQ)
         for c in range(NQ):
             row_scale_store(2, c * PIECE, PIECE, ENG2[c], rs[2])

@@ -24,7 +24,7 @@ S_SQ = (0, 1, 3)
 RECIP = (None, (3, 1), (3, 2))
 ENG1 = "vggg"
 NAT_BUFS = 2
-DEFER = 4
+DEFER = 3
 S_CHUNKS = ()
 S_CELLS = 128
 ENG0 = "aaaa"
@@ -35,7 +35,7 @@ STEP = 2
 FIRST = True
 V_EVACS = ()
 SQ_BUFS = 1
-MEM_BUFS = 4
+MEM_BUFS = 5
 LAG = 1
 LATE = (2, 3)
 NORM_AT = {0: -1, 1: -1, 2: 3, 3: 5}
@@ -106,7 +106,6 @@ def tile_contentaddressing_t_kernel(tc, memory, keys, betas, mask, out):
         beta_f = const.tile([P, HT], F32, name="beta_f")
         kn2 = const.tile([P, HT], F32, name="kn2")
         kn = const.tile([P, HT], F32, name="kn")
-        junk = const.tile([P, W], BF16, name="junk")
         kcodes = const.tile([P, HT * 512], U32, name="kcodes", align_bytes=64)
         kscale = const.tile([P, HT * 512], U8, name="kscale", align_bytes=64)
         s_all = [const.tile([P, C], F32, name="s%d" % t) for t in range(HT)]
@@ -124,7 +123,7 @@ def tile_contentaddressing_t_kernel(tc, memory, keys, betas, mask, out):
         flat = "p g h s -> p (g h s)"
 
         def mask_square(t):
-            m2 = head.tile([P, W], BF16, name="m2", bufs=HT)
+            m2 = head.tile([P, W], BF16, name="m2")
             m = mask_nat[t][:]
             nc.vector.tensor_tensor(out=m2[:], in0=m, in1=m, op=ALU.mult)
             mp[("h", t, 1)] = m2
@@ -142,10 +141,10 @@ def tile_contentaddressing_t_kernel(tc, memory, keys, betas, mask, out):
         def key_norm2(t):
             km = mp[("km", t)][:]
             if t in LATE:
-                nc.vector.scalar_tensor_tensor(out=junk[:], in0=km, scalar=1.0, in1=km, op0=ALU.mult, op1=ALU.mult,
+                nc.vector.scalar_tensor_tensor(out=km, in0=km, scalar=1.0, in1=km, op0=ALU.mult, op1=ALU.mult,
                                                accum_out=kn2[:, t:t + 1])
             else:
-                nc.scalar.activation(out=junk[:], in_=km, func=AF.Square, accum_out=kn2[:, t:t + 1])
+                nc.scalar.activation(out=s_all[t][:, C - CHUNK:C].bitcast(BF16), in_=km, func=AF.Square, accum_out=kn2[:, t:t + 1])
 
         def head_transposes(t, op):
             words = mp[("h", t, op)][:].bitcast(F32)
@@ -230,7 +229,7 @@ def tile_contentaddressing_t_kernel(tc, memory, keys, betas, mask, out):
             nc.scalar.activation(out=s_all[t][:, chunk_cols(k)], in_=mp[("mn2", t, k)][:], func=AF.Sqrt,
                                  bias=b_tiny[:], scale=1.0)
 
-        BANKS = (0, 2, 1, 3)
+        BANKS = (0, 1, 2, 3)
 
         for t in range(HT):
             mask_square(t)
@@ -346,7 +345,9 @@ def tile_contentaddressing_t_kernel(tc, memory, keys, betas, mask, out):
                                            op0=ALU.mult, op1=ALU.mult)
 
         def part_max(t, i, c0, cn):
-            nc.vector.tensor_reduce(out=pmx[t][:, i:i + 1], in_=s_all[t][:, c0:c0 + cn], axis=AX.X, op=ALU.min)
+            cols = s_all[t][:, c0:c0 + cn]
+            nc.vector.tensor_scalar(out=cols, in0=cols, scalar1=1.0, scalar2=None, op0=ALU.mult, op1=ALU.min,
+                                    accum_out=pmx[t][:, i:i + 1])
 
         def row_max(t, col, nq):
             nc.vector.tensor_reduce(out=mrow[t][:, col:col + 1], in_=pmx[t][:, 0:nq], axis=AX.X, op=ALU.min)

@@ -23,7 +23,8 @@ NQ = C // PIECE
 S_SQ = (0, 1, 3)
 RECIP = (None, (3, 1), (3, 2))
 ENG1 = "vggg"
-NAT_BUFS = 2
+NAT_BUFS = 3
+TB = 4
 DEFER = 3
 S_CHUNKS = ()
 S_CELLS = 128
@@ -31,7 +32,7 @@ ENG0 = "aaaa"
 HQ = 2
 COD = 2
 A1 = 4
-STEP = 2
+STEP = 4
 FIRST = True
 V_EVACS = ()
 SQ_BUFS = 1
@@ -39,7 +40,7 @@ MEM_BUFS = 5
 LAG = 1
 LATE = (2, 3)
 NORM_AT = {0: -1, 1: -1, 2: 3, 3: 5}
-KEY_STEPS = {1: 1, 3: 2, 5: 3}
+KEY_STEPS = {2: 1, 4: 2, 6: 3}
 ENG2 = "ggvv"
 EPS = 1e-8
 FLOPS = 2 * 2 * H * C * W
@@ -102,6 +103,8 @@ def tile_contentaddressing_t_kernel(tc, memory, keys, betas, mask, out):
         load_mem(1)
         for t in range(2, HT):
             load_head(keys_nat, keys2d, t)
+        for k in range(2, NAT_BUFS):
+            load_mem(k)
 
         beta_f = const.tile([P, HT], F32, name="beta_f")
         kn2 = const.tile([P, HT], F32, name="kn2")
@@ -111,14 +114,14 @@ def tile_contentaddressing_t_kernel(tc, memory, keys, betas, mask, out):
         s_all = [const.tile([P, C], F32, name="s%d" % t) for t in range(HT)]
         mem_codes = [const.tile([P, G * CHUNK], U32, name="mem_codes%d" % k, align_bytes=64) for k in range(NCH)]
         mem_scale = [const.tile([P, G * CHUNK], U8, name="mem_scale%d" % k, align_bytes=64) for k in range(NCH)]
-        hgrp = [const.tile([P, HT, G, P, 4], BF16, name="hgrp%d" % op, align_bytes=64) for op in range(2)]
+        hgrp = {}
         mp = {}
 
         def t_bank(shape, dtype):
-            return psum.tile(shape, dtype, name="tbank", tag="T")
+            return psum.tile(shape, dtype, name="tbank", tag="T", bufs=TB)
 
         def acc_bank(shape):
-            return psum.tile(shape, F32, name="acc", tag="acc")
+            return psum.tile(shape, F32, name="acc", tag="acc", bufs=8 - TB)
 
         flat = "p g h s -> p (g h s)"
 
@@ -152,6 +155,9 @@ def tile_contentaddressing_t_kernel(tc, memory, keys, betas, mask, out):
             for i in range(2 * G):
                 nc.tensor.transpose(out=xt[:, i, :], in_=words[:, i * P:(i + 1) * P], identity=ident_f[:])
             mp[("x", t, op)] = xt
+
+        def head_tile(op):
+            hgrp[op] = head.tile([P, HT, G, P, 4], BF16, name="hgrp", bufs=1, align_bytes=64)
 
         def head_evac(t, op):
             copy = nc.vector.tensor_copy if (t, op) in V_EVACS else nc.scalar.copy
@@ -231,6 +237,7 @@ def tile_contentaddressing_t_kernel(tc, memory, keys, betas, mask, out):
 
         BANKS = (0, 1, 2, 3)
 
+        head_tile(1)
         for t in range(HT):
             mask_square(t)
             head_transposes(t, 1)
@@ -254,6 +261,7 @@ def tile_contentaddressing_t_kernel(tc, memory, keys, betas, mask, out):
             mem_transposes(1, b)
         for b in BANKS:
             mem_evac(1, b)
+        head_tile(0)
         head_transposes(0, 0)
         head_evac(0, 0)
         for t in range(HT):
@@ -261,8 +269,8 @@ def tile_contentaddressing_t_kernel(tc, memory, keys, betas, mask, out):
                 key_norm2(t)
 
         for k in range(NCH):
-            if k + 2 < NCH:
-                load_mem(k + 2)
+            if k + NAT_BUFS < NCH:
+                load_mem(k + NAT_BUFS)
             if k in KEY_STEPS:
                 t = KEY_STEPS[k]
                 head_transposes(t, 0)

@@ -20,12 +20,12 @@ NCH = C // CHUNK
 G = W // 512
 PIECE = 1024
 NQ = C // PIECE
-S_SQ = (0, 1, 3)
+S_SQ = (0, 1, 3, 5, 7)
 RECIP = (None, (3, 1), (3, 2))
-ENG1 = "vggg"
+ENG1 = "gggg"
 NAT_BUFS = 3
 TB = 4
-DEFER = 3
+DEFER = 5
 S_CHUNKS = ()
 S_CELLS = 128
 ENG0 = "aaaa"
@@ -308,11 +308,11 @@ def tile_contentaddressing_t_kernel(tc, memory, keys, betas, mask, out):
                 key_mask2(t_next)
         early = HT - len(LATE)
         nc.scalar.activation(out=kn[:, 0:early], in_=kn2[:, 0:early], func=AF.Sqrt, bias=b_tiny[:], scale=1.0)
-        head_quant(0, HT, 0)
         for k in range(DEFER, NCH):
             mem_quant(k)
         for t in LATE:
             key_norm2(t)
+        head_quant(0, HT, 0)
 
         HALF = C // 2
         last = HT - 1

@@ -15,39 +15,21 @@ AX = mybir.AxisListType
 P = 128
 H, C, W = 512, 4096, 1024
 HT = H // P
+LAST = HT - 1
 CHUNK = 512
 NCH = C // CHUNK
 G = W // 512
+HALF = C // 2
 PIECE = 1024
 NQ = C // PIECE
-S_SQ = (0, 1, 3, 5, 7)
-RECIP = (None, (3, 1), (3, 2))
-ENG1 = "gggg"
-NAT_BUFS = 3
-TB = 4
-DEFER = 5
-S_CHUNKS = ()
-S_CELLS = 128
-ENG0 = "aaaa"
-HQ = 2
-COD = 2
-A1 = 4
-STEP = 4
-FIRST = True
-V_EVACS = ()
-SQ_BUFS = 1
-MEM_BUFS = 5
-LAG = 1
-LATE = (2, 3)
-NORM_AT = {0: -1, 1: -1, 2: 3, 3: 5}
-KEY_STEPS = {2: 1, 4: 2, 6: 3}
-ENG2 = "ggvv"
+WORDS = G * P
+DOTS, NORM = 0, 1
+LATE_MEM = 5
+SCALAR_HALF = (0, 1, 7)
+TWICE = (4, 10)
 EPS = 1e-8
+TINY = 1e-34
 FLOPS = 2 * 2 * H * C * W
-
-
-def s_cells(k):
-    return S_CELLS if k in S_CHUNKS else 0
 
 
 def tile_contentaddressing_t_kernel(tc, memory, keys, betas, mask, out):
@@ -59,16 +41,16 @@ def tile_contentaddressing_t_kernel(tc, memory, keys, betas, mask, out):
 
     with ExitStack() as ctx:
         const = ctx.enter_context(tc.tile_pool(name="const", bufs=1))
-        natp = ctx.enter_context(tc.tile_pool(name="natp", bufs=NAT_BUFS))
-        grp = ctx.enter_context(tc.tile_pool(name="grp", bufs=2))
-        memp = ctx.enter_context(tc.tile_pool(name="memp", bufs=MEM_BUFS))
+        natp = ctx.enter_context(tc.tile_pool(name="natp", bufs=3))
+        grp = ctx.enter_context(tc.tile_pool(name="grp", bufs=1))
+        memp = ctx.enter_context(tc.tile_pool(name="memp", bufs=5))
         head = ctx.enter_context(tc.tile_pool(name="head", bufs=2))
-        cod = ctx.enter_context(tc.tile_pool(name="cod", bufs=COD))
+        cod = ctx.enter_context(tc.tile_pool(name="cod", bufs=2))
         psum = ctx.enter_context(tc.psum_pool(name="psum", bufs=4))
         ctx.enter_context(tc.manual_schedule())
 
         b_tiny = const.tile([P, 1], F32, name="b_tiny")
-        nc.vector.memset(b_tiny[:], 1e-34)
+        nc.vector.memset(b_tiny[:], TINY)
         b_eps = const.tile([P, 1], F32, name="b_eps")
         nc.vector.memset(b_eps[:], EPS)
         warm = const.tile([P, 1], F32, name="warm")
@@ -82,129 +64,110 @@ def tile_contentaddressing_t_kernel(tc, memory, keys, betas, mask, out):
 
         keys_nat = [const.tile([P, W], BF16, name="keys_nat%d" % t) for t in range(HT)]
         mask_nat = [const.tile([P, W], BF16, name="mask_nat%d" % t) for t in range(HT)]
-        nat = {}
+        mem_nat = {}
 
         def load_head(dst, src, t):
             nc.sync.dma_start(out=dst[t][:], in_=src[t * P:(t + 1) * P, :])
 
         def load_mem(k):
-            t_nat = natp.tile([P, 4, W], BF16, name="mem_nat")
+            mem_nat[k] = natp.tile([P, 4, W], BF16, name="mem_nat")
             view = mem2d[k * CHUNK:(k + 1) * CHUNK, :].rearrange("(j p) w -> p j w", p=P)
-            for j in range(0, 4, 2):
-                nc.sync.dma_start(out=t_nat[:, j:j + 2, :], in_=view[:, j:j + 2, :])
-            nat[k] = t_nat
+            for j in (0, 2):
+                nc.sync.dma_start(out=mem_nat[k][:, j:j + 2, :], in_=view[:, j:j + 2, :])
 
         nc.scalar.dma_start(out=brow[0:HT, :], in_=betas.rearrange("o (t p) -> (o t) p", p=P))
         for t in range(HT):
             load_head(mask_nat, mask2d, t)
-        for t in range(2):
+        for t in (0, 1):
             load_head(keys_nat, keys2d, t)
         load_mem(0)
         load_mem(1)
-        for t in range(2, HT):
+        for t in (2, 3):
             load_head(keys_nat, keys2d, t)
-        for k in range(2, NAT_BUFS):
-            load_mem(k)
+        load_mem(2)
 
-        beta_f = const.tile([P, HT], F32, name="beta_f")
+        beta_neg = const.tile([P, HT], F32, name="beta_neg")
         kn2 = const.tile([P, HT], F32, name="kn2")
         kn = const.tile([P, HT], F32, name="kn")
-        kcodes = const.tile([P, HT * 512], U32, name="kcodes", align_bytes=64)
-        kscale = const.tile([P, HT * 512], U8, name="kscale", align_bytes=64)
+        key_codes = const.tile([P, 2 * HT * WORDS], U32, name="key_codes", align_bytes=64)
+        key_scale = const.tile([P, 2 * HT * WORDS], U8, name="key_scale", align_bytes=64)
         s_all = [const.tile([P, C], F32, name="s%d" % t) for t in range(HT)]
         mem_codes = [const.tile([P, G * CHUNK], U32, name="mem_codes%d" % k, align_bytes=64) for k in range(NCH)]
         mem_scale = [const.tile([P, G * CHUNK], U8, name="mem_scale%d" % k, align_bytes=64) for k in range(NCH)]
-        hgrp = {}
-        mp = {}
+        km, head_nat, head_t, head_grp = {}, {}, {}, {}
+        mem_t, mem_grp, sq_grp, sq_codes = {}, {}, {}, {}
 
-        def t_bank(shape, dtype):
-            return psum.tile(shape, dtype, name="tbank", tag="T", bufs=TB)
+        def t_bank(shape):
+            return psum.tile(shape, F32, name="tbank", tag="T")
 
         def acc_bank(shape):
-            return psum.tile(shape, F32, name="acc", tag="acc", bufs=8 - TB)
-
-        flat = "p g h s -> p (g h s)"
+            return psum.tile(shape, F32, name="acc", tag="acc")
 
         def mask_square(t):
-            m2 = head.tile([P, W], BF16, name="m2")
+            m2 = head_nat[t, NORM] = head.tile([P, W], BF16, name="m2")
             m = mask_nat[t][:]
             nc.vector.tensor_tensor(out=m2[:], in0=m, in1=m, op=ALU.mult)
-            mp[("h", t, 1)] = m2
 
         def key_mask(t):
-            km = head.tile([P, W], F32, name="km")
-            nc.vector.tensor_tensor(out=km[:], in0=keys_nat[t][:], in1=mask_nat[t][:], op=ALU.mult)
-            mp[("km", t)] = km
+            km[t] = head.tile([P, W], F32, name="km")
+            nc.vector.tensor_tensor(out=km[t][:], in0=keys_nat[t][:], in1=mask_nat[t][:], op=ALU.mult)
 
         def key_mask2(t):
-            km2 = head.tile([P, W], BF16, name="km2")
-            nc.vector.tensor_tensor(out=km2[:], in0=mp[("km", t)][:], in1=mask_nat[t][:], op=ALU.mult)
-            mp[("h", t, 0)] = km2
+            km2 = head_nat[t, DOTS] = head.tile([P, W], BF16, name="km2")
+            nc.vector.tensor_tensor(out=km2[:], in0=km[t][:], in1=mask_nat[t][:], op=ALU.mult)
 
-        def key_norm2(t):
-            km = mp[("km", t)][:]
-            if t in LATE:
-                nc.vector.scalar_tensor_tensor(out=km, in0=km, scalar=1.0, in1=km, op0=ALU.mult, op1=ALU.mult,
-                                               accum_out=kn2[:, t:t + 1])
-            else:
-                nc.scalar.activation(out=s_all[t][:, C - CHUNK:C].bitcast(BF16), in_=km, func=AF.Square, accum_out=kn2[:, t:t + 1])
+        def key_norm2_scalar(t):
+            unused = s_all[t][:, C - CHUNK:C].bitcast(BF16)
+            nc.scalar.activation(out=unused, in_=km[t][:], func=AF.Square, accum_out=kn2[:, t:t + 1])
+
+        def key_norm2_vector(t):
+            nc.vector.scalar_tensor_tensor(out=km[t][:], in0=km[t][:], scalar=1.0, in1=km[t][:], op0=ALU.mult,
+                                           op1=ALU.mult, accum_out=kn2[:, t:t + 1])
 
         def head_transposes(t, op):
-            words = mp[("h", t, op)][:].bitcast(F32)
-            xt = acc_bank([P, 2 * G, P])
+            words = head_nat[t, op][:].bitcast(F32)
+            head_t[t, op] = acc_bank([P, 2 * G, P])
             for i in range(2 * G):
-                nc.tensor.transpose(out=xt[:, i, :], in_=words[:, i * P:(i + 1) * P], identity=ident_f[:])
-            mp[("x", t, op)] = xt
+                nc.tensor.transpose(out=head_t[t, op][:, i, :], in_=words[:, i * P:(i + 1) * P], identity=ident_f[:])
 
-        def head_tile(op):
-            hgrp[op] = head.tile([P, HT, G, P, 4], BF16, name="hgrp", bufs=1, align_bytes=64)
+        def head_group(op):
+            head_grp[op] = head.tile([P, HT, G, P, 4], BF16, name="head_grp", bufs=1, align_bytes=64)
 
         def head_evac(t, op):
-            copy = nc.vector.tensor_copy if (t, op) in V_EVACS else nc.scalar.copy
-            copy(out=hgrp[op][:, t].bitcast(F32), in_=mp[("x", t, op)][:].rearrange("p (g u) h -> p g h u", u=2))
+            nc.scalar.copy(out=head_grp[op][:, t].bitcast(F32),
+                           in_=head_t[t, op][:].rearrange("p (g u) h -> p g h u", u=2))
 
         def head_quant(t, n, op):
-            cs = slice(op * HT * 256 + t * 256, op * HT * 256 + (t + n) * 256)
-            nc.vector.quantize_mx(out=kcodes[:, cs].bitcast(FP8X4), scales=kscale[:, cs],
-                                  in_=hgrp[op][:, t:t + n].rearrange("p t g h s -> p (t g h s)"))
+            cs = slice((op * HT + t) * WORDS, (op * HT + t + n) * WORDS)
+            nc.vector.quantize_mx(out=key_codes[:, cs].bitcast(FP8X4), scales=key_scale[:, cs],
+                                  in_=head_grp[op][:, t:t + n].rearrange("p t g h s -> p (t g h s)"))
 
         def mem_transposes(k, b):
             g, half = divmod(b, 2)
-            memf = nat[k][:].bitcast(F32)
-            tb = t_bank([P, 2, 256], F32)
+            words = mem_nat[k][:].bitcast(F32)
+            bank = mem_t[k, b] = t_bank([P, 2, 256])
             for jj in range(2):
                 for u in range(2):
                     i = 2 * g + u
-                    nc.tensor.transpose(
-                        out=tb[:, u, jj * P:(jj + 1) * P],
-                        in_=memf[:, 2 * half + jj, i * P:(i + 1) * P],
-                        identity=ident_f[:])
-            mp[(k, "tb", b)] = tb
+                    nc.tensor.transpose(out=bank[:, u, jj * P:(jj + 1) * P],
+                                        in_=words[:, 2 * half + jj, i * P:(i + 1) * P], identity=ident_f[:])
 
         def mem_evac(k, b):
             g, half = divmod(b, 2)
-            if b == BANKS[0]:
-                mp[(k, "mem")] = memp.tile([P, G, CHUNK, 4], BF16, name="mem_grp", align_bytes=64)
-                mp[(k, "sq")] = grp.tile([P, G, CHUNK, 4], BF16, name="sq_grp", bufs=SQ_BUFS, align_bytes=64)
-            nc.scalar.copy(out=mp[(k, "mem")][:].bitcast(F32)[:, g, 256 * half:256 * half + 256, :],
-                           in_=mp[(k, "tb", b)][:].rearrange("p u r -> p r u"))
-            n = s_cells(k)
-            if b == 0 and n:
-                nc.scalar.activation(
-                    out=mp[(k, "sq")][:, 0, 0:n, :].rearrange("p r (u e) -> p r u e", e=2),
-                    in_=mp[(k, "tb", b)][:, :, 0:n].bitcast(BF16).rearrange("p u (r e) -> p r u e", e=2),
-                    func=AF.Square)
+            if b == 0:
+                mem_grp[k] = memp.tile([P, G, CHUNK, 4], BF16, name="mem_grp", align_bytes=64)
+                sq_grp[k] = grp.tile([P, G, CHUNK, 4], BF16, name="sq_grp", align_bytes=64)
+            nc.scalar.copy(out=mem_grp[k][:].bitcast(F32)[:, g, 256 * half:256 * half + 256, :],
+                           in_=mem_t[k, b][:].rearrange("p u r -> p r u"))
 
         def mem_square(k):
             for g in range(G):
-                c0 = s_cells(k) if g == 0 else 0
-                m = mp[(k, "mem")][:, g, c0:, :].rearrange("p c s -> p (c s)")
-                nc.vector.tensor_tensor(out=mp[(k, "sq")][:, g, c0:, :].rearrange("p c s -> p (c s)"),
-                                        in0=m, in1=m, op=ALU.mult)
+                m = mem_grp[k][:, g].rearrange("p c s -> p (c s)")
+                nc.vector.tensor_tensor(out=sq_grp[k][:, g].rearrange("p c s -> p (c s)"), in0=m, in1=m, op=ALU.mult)
 
         def mem_quant(k):
             nc.vector.quantize_mx(out=mem_codes[k][:].bitcast(FP8X4), scales=mem_scale[k][:],
-                                  in_=mp[(k, "mem")][:].rearrange(flat))
+                                  in_=mem_grp[k][:].rearrange("p g c s -> p (g c s)"))
 
         def sq_quant(k):
             dat = cod.tile([P, G * CHUNK], U32, name="sq_codes", align_bytes=64)
@@ -212,238 +175,236 @@ def tile_contentaddressing_t_kernel(tc, memory, keys, betas, mask, out):
             for g in range(G):
                 gs = slice(g * CHUNK, (g + 1) * CHUNK)
                 nc.vector.quantize_mx(out=dat[:, gs].bitcast(FP8X4), scales=scl[:, gs],
-                                      in_=mp[(k, "sq")][:, g].rearrange("p c s -> p (c s)"))
-            mp[(k, "sqq")] = (dat, scl)
+                                      in_=sq_grp[k][:, g].rearrange("p c s -> p (c s)"))
+            sq_codes[k] = (dat, scl)
 
-        def product(t, k, op, acc):
-            dat, scl = (mem_codes[k], mem_scale[k]) if op == 0 else mp[(k, "sqq")]
+        def product(t, k, op, bank):
+            dat, scl = (mem_codes[k], mem_scale[k]) if op == DOTS else sq_codes[k]
             for g in range(G):
-                c0 = op * HT * 256 + t * 256 + g * P
-                nc.tensor.matmul_mx(
-                    out=acc[:],
-                    lhsT=kcodes[:, c0:c0 + P].bitcast(FP8X4),
-                    lhsT_scale=kscale[:, c0:c0 + P],
-                    rhs=dat[:, g * CHUNK:(g + 1) * CHUNK].bitcast(FP8X4),
-                    rhs_scale=scl[:, g * CHUNK:(g + 1) * CHUNK],
-                    start=(g == 0), stop=(g == G - 1))
-            return acc
+                c0 = (op * HT + t) * WORDS + g * P
+                gs = slice(g * CHUNK, (g + 1) * CHUNK)
+                nc.tensor.matmul_mx(out=bank[:],
+                                    lhsT=key_codes[:, c0:c0 + P].bitcast(FP8X4), lhsT_scale=key_scale[:, c0:c0 + P],
+                                    rhs=dat[:, gs].bitcast(FP8X4), rhs_scale=scl[:, gs],
+                                    start=(g == 0), stop=(g == G - 1))
 
-        def chunk_cols(k):
-            return slice(k * CHUNK, (k + 1) * CHUNK)
+        def cells(t, k):
+            return s_all[t][:, k * CHUNK:(k + 1) * CHUNK]
 
-        def norm_root(t, k):
-            nc.scalar.activation(out=s_all[t][:, chunk_cols(k)], in_=mp[("mn2", t, k)][:], func=AF.Sqrt,
-                                 bias=b_tiny[:], scale=1.0)
+        def mem_norm(t, k):
+            bank = acc_bank([P, CHUNK])
+            product(t, k, NORM, bank)
+            nc.scalar.activation(out=cells(t, k), in_=bank[:], func=AF.Sqrt, bias=b_tiny[:], scale=1.0)
 
-        BANKS = (0, 1, 2, 3)
-
-        head_tile(1)
+        head_group(NORM)
         for t in range(HT):
             mask_square(t)
-            head_transposes(t, 1)
-            head_evac(t, 1)
-        bT = t_bank([P, P], F32)
-        nc.tensor.transpose(out=bT[:].bitcast(BF16)[:, 0:P], in_=brow[:], identity=ident_b[:])
-        for b in BANKS[0:3]:
+            head_transposes(t, NORM)
+            head_evac(t, NORM)
+        beta_t = t_bank([P, P])[:].bitcast(BF16)
+        nc.tensor.transpose(out=beta_t[:, 0:P], in_=brow[:], identity=ident_b[:])
+        for b in range(3):
             mem_transposes(0, b)
-        nc.vector.tensor_scalar(out=beta_f[:], in0=bT[:].bitcast(BF16)[:, 0:HT], scalar1=-1.0, scalar2=None, op0=ALU.mult)
-        mem_transposes(0, BANKS[3])
+        nc.vector.tensor_scalar(out=beta_neg[:], in0=beta_t[:, 0:HT], scalar1=-1.0, scalar2=None, op0=ALU.mult)
+        mem_transposes(0, 3)
         key_mask(0)
         key_mask(1)
-        for b in BANKS:
+        for b in range(4):
             mem_evac(0, b)
         key_mask2(0)
-        for t in range(0, HT, HQ):
-            head_quant(t, HQ, 1)
+        head_quant(0, 2, NORM)
+        head_quant(2, 2, NORM)
         mem_square(0)
         sq_quant(0)
-        for b in BANKS:
+        for b in range(4):
             mem_transposes(1, b)
-        for b in BANKS:
+        for b in range(4):
             mem_evac(1, b)
-        head_tile(0)
-        head_transposes(0, 0)
-        head_evac(0, 0)
-        for t in range(HT):
-            if NORM_AT[t] == -1:
-                key_norm2(t)
+        head_group(DOTS)
+        head_transposes(0, DOTS)
+        head_evac(0, DOTS)
+        key_norm2_scalar(0)
+        key_norm2_scalar(1)
 
         for k in range(NCH):
-            if k + NAT_BUFS < NCH:
-                load_mem(k + NAT_BUFS)
-            if k in KEY_STEPS:
-                t = KEY_STEPS[k]
-                head_transposes(t, 0)
-            for h in range(0, HT, STEP):
-                if k + 2 < NCH and FIRST:
-                    for b in BANKS[h:h + STEP]:
-                        mem_transposes(k + 2, b)
-                    for b in BANKS[h:h + STEP]:
-                        mem_evac(k + 2, b)
-                for t in range(h, h + STEP):
-                    mp[("mn2", t, k)] = product(t, k, 1, acc_bank([P, CHUNK]))
-                    norm_root(t, k)
-                if k + 2 < NCH and not FIRST:
-                    for b in BANKS[h:h + STEP]:
-                        mem_transposes(k + 2, b)
-                    for b in BANKS[h:h + STEP]:
-                        mem_evac(k + 2, b)
-            if k in KEY_STEPS:
-                t = KEY_STEPS[k]
-                head_evac(t, 0)
+            key_tile = k // 2 if k in (2, 4, 6) else None
+            if k + 3 < NCH:
+                load_mem(k + 3)
+            if key_tile:
+                head_transposes(key_tile, DOTS)
+            if k + 2 < NCH:
+                for b in range(4):
+                    mem_transposes(k + 2, b)
+                for b in range(4):
+                    mem_evac(k + 2, b)
             for t in range(HT):
-                if NORM_AT[t] == k and t not in LATE:
-                    key_norm2(t)
+                mem_norm(t, k)
+            if key_tile:
+                head_evac(key_tile, DOTS)
+            if k == 3:
+                key_norm2_scalar(2)
             if k + 1 < NCH:
                 mem_square(k + 1)
                 sq_quant(k + 1)
-            t_next = KEY_STEPS[k] + 1 if k in KEY_STEPS else HT
-            if t_next < HT:
-                key_mask(t_next)
-            if k + 1 - LAG < DEFER:
-                mem_quant(k + 1 - LAG)
+            if k in (2, 4):
+                key_mask(key_tile + 1)
+            if k < LATE_MEM:
+                mem_quant(k)
             if k == 0:
                 key_mask2(1)
-            if t_next < HT:
-                key_mask2(t_next)
-        early = HT - len(LATE)
-        nc.scalar.activation(out=kn[:, 0:early], in_=kn2[:, 0:early], func=AF.Sqrt, bias=b_tiny[:], scale=1.0)
-        for k in range(DEFER, NCH):
+            if k == 1:
+                head_quant(0, 1, DOTS)
+            if k in (2, 4):
+                key_mask2(key_tile + 1)
+        nc.scalar.activation(out=kn[:, 0:LAST], in_=kn2[:, 0:LAST], func=AF.Sqrt, bias=b_tiny[:], scale=1.0)
+        for k in range(LATE_MEM, NCH):
             mem_quant(k)
-        for t in LATE:
-            key_norm2(t)
-        head_quant(0, HT, 0)
+        key_norm2_vector(LAST)
+        head_quant(1, 1, DOTS)
+        head_quant(2, 2, DOTS)
 
-        HALF = C // 2
-        last = HT - 1
-        pmx = [const.tile([P, NQ], F32, name="pmx%d" % t) for t in range(HT)]
-        mrow = [const.tile([P, 2], F32, name="mrow%d" % t) for t in range(HT)]
+        part = [const.tile([P, NQ], F32, name="part%d" % t) for t in range(HT)]
+        low = [const.tile([P, 2], F32, name="low%d" % t) for t in range(HT)]
         sums = [const.tile([P, 1], F32, name="sums%d" % t) for t in range(HT)]
         sums_a = const.tile([P, 1], F32, name="sums_a")
         fold = const.tile([P, 1], F32, name="fold")
         rs = [const.tile([P, 1], F32, name="rs%d" % t) for t in range(HT)]
-        rk = {t: const.tile([P, 1], F32, name="rk%d" % t) for t in LATE}
+        rk = const.tile([P, 1], F32, name="rk")
         rs_a = const.tile([P, 1], F32, name="rs_a")
+        dots, copies = {}, {}
 
-        def piece(t, q):
-            return s_all[t][:, q * PIECE:(q + 1) * PIECE]
+        def piece(i, c0=0, c1=PIECE):
+            t, q = divmod(i, NQ)
+            return s_all[t][:, q * PIECE + c0:q * PIECE + c1]
 
-        def root_recip(i, n):
-            t, c0 = divmod(i * CHUNK, C)
-            cols = s_all[t][:, c0:c0 + n * CHUNK]
-            nc.scalar.activation(out=cols, in_=cols, func=AF.Abs_reciprocal_sqrt,
-                                 bias=b_eps[:], scale=kn[:, t:t + 1])
+        def root_recip(t, c0, cn):
+            cols = s_all[t][:, c0:c0 + cn]
+            nc.scalar.activation(out=cols, in_=cols, func=AF.Abs_reciprocal_sqrt, bias=b_eps[:],
+                                 scale=kn[:, t:t + 1])
 
         def scalar_square(i):
-            t, q = divmod(i, NQ)
-            a = piece(t, q)[:, 0:CHUNK]
-            if i in S_SQ:
+            if i in SCALAR_HALF:
+                a = piece(i, 0, CHUNK)
                 nc.scalar.activation(out=a, in_=a, func=AF.Square)
 
         def gpsimd_square(i):
-            t, q = divmod(i, NQ)
-            b = piece(t, q)[:, CHUNK if i in S_SQ else 0:]
-            nc.gpsimd.tensor_tensor(out=b, in0=b, in1=b, op=ALU.mult)
+            if i not in TWICE:
+                a = piece(i, CHUNK if i in SCALAR_HALF else 0)
+                nc.gpsimd.tensor_tensor(out=a, in0=a, in1=a, op=ALU.mult)
+
+        def dots_product(t, k):
+            dots[t, k] = acc_bank([P, CHUNK]) if k % 2 == 0 else t_bank([P, CHUNK])
+            product(t, k, DOTS, dots[t, k])
+
+        def recip_copy(t, k):
+            copies[t, k] = t_bank([P, CHUNK]) if k % 2 == 0 else acc_bank([P, CHUNK])
+            nc.tensor.matmul(out=copies[t, k][:], lhsT=ident_f[:], rhs=cells(t, k), start=True, stop=True)
 
         def score(t, k):
-            bank = acc_bank([P, CHUNK]) if k % 2 == 0 else t_bank([P, CHUNK], F32)
-            product(t, k, 0, bank)
-            col = s_all[t][:, chunk_cols(k)]
-            nc.vector.scalar_tensor_tensor(out=col, in0=bank[:], scalar=beta_f[:, t:t + 1], in1=col,
+            nc.vector.scalar_tensor_tensor(out=cells(t, k), in0=dots[t, k][:], scalar=beta_neg[:, t:t + 1],
+                                           in1=cells(t, k), op0=ALU.mult, op1=ALU.mult)
+
+        def second_factor(t, k):
+            nc.vector.scalar_tensor_tensor(out=cells(t, k), in0=copies[t, k][:], scalar=1.0, in1=cells(t, k),
                                            op0=ALU.mult, op1=ALU.mult)
 
-        def part_max(t, i, c0, cn):
+        def part_min(t, i, c0, cn):
             cols = s_all[t][:, c0:c0 + cn]
             nc.vector.tensor_scalar(out=cols, in0=cols, scalar1=1.0, scalar2=None, op0=ALU.mult, op1=ALU.min,
-                                    accum_out=pmx[t][:, i:i + 1])
+                                    accum_out=part[t][:, i:i + 1])
 
-        def row_max(t, col, nq):
-            nc.vector.tensor_reduce(out=mrow[t][:, col:col + 1], in_=pmx[t][:, 0:nq], axis=AX.X, op=ALU.min)
+        def row_min(t, col, n):
+            nc.vector.tensor_reduce(out=low[t][:, col:col + 1], in_=part[t][:, 0:n], axis=AX.X, op=ALU.min)
 
         def row_exp(t, c0, cn, col, total):
-            nc.scalar.activation(out=s_all[t][:, c0:c0 + cn], in_=s_all[t][:, c0:c0 + cn], func=AF.Exp,
-                                 bias=mrow[t][:, col:col + 1], scale=-1.0, accum_out=total[:])
+            cols = s_all[t][:, c0:c0 + cn]
+            nc.scalar.activation(out=cols, in_=cols, func=AF.Exp, bias=low[t][:, col:col + 1], scale=-1.0,
+                                 accum_out=total[:])
 
         def row_recip(t):
             nc.vector.reciprocal(out=rs[t][:], in_=sums[t][:])
 
-        def row_scale_store(t, c0, cn, eng, by):
+        def scale_store(t, c0, cn, eng, by):
             cols = s_all[t][:, c0:c0 + cn]
             if eng == "v":
                 nc.vector.tensor_scalar(out=cols, in0=cols, scalar1=by[:], scalar2=None, op0=ALU.mult)
-            elif eng == "a":
+            elif eng == "s":
                 nc.scalar.activation(out=cols, in_=cols, func=AF.Copy, scale=by[:])
             else:
                 nc.gpsimd.tensor_scalar(out=cols, in0=cols, scalar1=by[:], scalar2=0.0, op0=ALU.mult, op1=ALU.add)
             nc.sync.dma_start(out=out2d[t * P:(t + 1) * P, c0:c0 + cn], in_=cols)
 
-        def recip0():
-            row_recip(0)
-            for c in range(NQ):
-                row_scale_store(0, c * PIECE, PIECE, ENG0[c], rs[0])
-            row_exp(1, 0, C, 0, sums[1])
-
-        def late_root(t):
-            nc.scalar.activation(out=rk[t][:], in_=kn2[:, t:t + 1], func=AF.Abs_reciprocal_sqrt, bias=b_tiny[:], scale=1.0)
-
-        def late_norm(t):
-            nc.scalar.activation(out=kn[:, t:t + 1], in_=kn2[:, t:t + 1], func=AF.Copy, scale=rk[t][:])
+        def scale_store_row(t, engines):
+            for q, eng in enumerate(engines):
+                scale_store(t, q * PIECE, PIECE, eng, rs[t])
 
         for i in range(HT * NQ):
+            t, q = divmod(i, NQ)
             if i < 2:
-                root_recip(2 * i, 1)
-                root_recip(2 * i + 1, 1)
+                root_recip(t, q * PIECE, CHUNK)
+                root_recip(t, q * PIECE + CHUNK, CHUNK)
                 scalar_square(i)
-            elif i % 2 == 0:
-                if i // NQ + 1 in LATE:
-                    (late_root if i % NQ == 0 else late_norm)(i // NQ + 1)
-                if i < A1:
-                    root_recip(2 * i, 2)
-                    root_recip(2 * i + 2, 2)
+            elif q % 2 == 0:
+                if t == LAST - 1 and q == 0:
+                    nc.scalar.activation(out=rk[:], in_=kn2[:, LAST:HT], func=AF.Abs_reciprocal_sqrt,
+                                         bias=b_tiny[:], scale=1.0)
+                if t == LAST - 1 and q == 2:
+                    nc.scalar.activation(out=kn[:, LAST:HT], in_=kn2[:, LAST:HT], func=AF.Copy, scale=rk[:])
+                if i == 2:
+                    root_recip(t, q * PIECE, PIECE)
+                    root_recip(t, (q + 1) * PIECE, PIECE)
                 else:
-                    root_recip(2 * i, 4)
+                    root_recip(t, q * PIECE, 2 * PIECE)
                 scalar_square(i)
                 scalar_square(i + 1)
             gpsimd_square(i)
 
         for t in range(HT):
             for q in range(NQ):
+                dots_product(t, 2 * q)
+                dots_product(t, 2 * q + 1)
+                if t * NQ + q in TWICE:
+                    recip_copy(t, 2 * q)
+                    recip_copy(t, 2 * q + 1)
                 score(t, 2 * q)
                 if q == 0 and t >= 1:
-                    part_max(t - 1, 1, HALF, HALF)
+                    part_min(t - 1, 1, HALF, HALF)
                 if q == 2:
-                    part_max(t, 0, 0, HALF)
-                if q == 3 and t == last:
-                    part_max(t, 1, HALF, PIECE)
+                    part_min(t, 0, 0, HALF)
+                if q == 3 and t == LAST:
+                    part_min(t, 1, HALF, PIECE)
                 score(t, 2 * q + 1)
+                if t * NQ + q in TWICE:
+                    second_factor(t, 2 * q)
+                    second_factor(t, 2 * q + 1)
                 if q == 0 and t >= 1:
-                    row_max(t - 1, 0, 2)
+                    row_min(t - 1, 0, 2)
                     if t != 2:
                         row_exp(t - 1, 0, C, 0, sums[t - 1])
-                if q == 1 and t == 2:
-                    recip0()
-                if t == last and q == 2:
-                    row_max(t, 0, 1)
-                if (t, q) == RECIP[1]:
+                if t == 2 and q == 1:
+                    row_recip(0)
+                    scale_store_row(0, "ssss")
+                    row_exp(1, 0, C, 0, sums[1])
+                if t == LAST and q == 1:
                     row_recip(1)
-                    for c in range(NQ):
-                        row_scale_store(1, c * PIECE, PIECE, ENG1[c], rs[1])
-                if (t, q) == RECIP[2]:
+                    scale_store_row(1, "gggg")
+                if t == LAST and q == 2:
+                    row_min(t, 0, 1)
                     row_recip(2)
                     row_exp(t, 0, HALF, 0, sums_a)
-        part_max(last, 2, C - PIECE, CHUNK)
-        part_max(last, 3, C - CHUNK, CHUNK)
-        row_max(last, 1, NQ)
-        for c in range(NQ):
-            row_scale_store(2, c * PIECE, PIECE, ENG2[c], rs[2])
-        nc.scalar.activation(out=fold[:], in_=mrow[last][:, 0:1], func=AF.Exp, bias=mrow[last][:, 1:2], scale=-1.0)
-        row_exp(last, HALF, HALF, 1, sums[last])
-        nc.vector.scalar_tensor_tensor(out=sums[last][:], in0=sums_a[:], scalar=fold[:], in1=sums[last][:],
+        part_min(LAST, 2, C - PIECE, CHUNK)
+        part_min(LAST, 3, C - CHUNK, CHUNK)
+        row_min(LAST, 1, NQ)
+        scale_store_row(2, "ggvv")
+
+        nc.scalar.activation(out=fold[:], in_=low[LAST][:, 0:1], func=AF.Exp, bias=low[LAST][:, 1:2], scale=-1.0)
+        row_exp(LAST, HALF, HALF, 1, sums[LAST])
+        nc.vector.scalar_tensor_tensor(out=sums[LAST][:], in0=sums_a[:], scalar=fold[:], in1=sums[LAST][:],
                                        op0=ALU.mult, op1=ALU.add)
-        row_recip(last)
-        row_scale_store(last, HALF, 512, "v", rs[last])
-        nc.vector.tensor_tensor(out=rs_a[:], in0=rs[last][:], in1=fold[:], op=ALU.mult)
-        row_scale_store(last, HALF + 512, 512, "v", rs[last])
-        row_scale_store(last, HALF + 1024, 1024, "v", rs[last])
-        row_scale_store(last, 0, 1024, "v", rs_a)
-        row_scale_store(last, 1024, 1024, "v", rs_a)
+        row_recip(LAST)
+        scale_store(LAST, HALF, CHUNK, "v", rs[LAST])
+        nc.vector.tensor_tensor(out=rs_a[:], in0=rs[LAST][:], in1=fold[:], op=ALU.mult)
+        scale_store(LAST, HALF + CHUNK, CHUNK, "v", rs[LAST])
+        scale_store(LAST, HALF + PIECE, PIECE, "v", rs[LAST])
+        scale_store(LAST, 0, PIECE, "v", rs_a)
+        scale_store(LAST, PIECE, PIECE, "v", rs_a)

from contextlib import ExitStack

import concourse.mybir as mybir
from concourse.masks import make_identity

F32 = mybir.dt.float32
BF16 = mybir.dt.bfloat16
U32 = mybir.dt.uint32
U8 = mybir.dt.uint8
FP8X4 = mybir.dt.float8_e4m3fn_x4
AF = mybir.ActivationFunctionType
ALU = mybir.AluOpType
AX = mybir.AxisListType

P = 128
H, C, W = 512, 4096, 1024
HT = H // P
LAST = HT - 1
CHUNK = 512
NCH = C // CHUNK
G = W // 512
HALF = C // 2
PIECE = 1024
NQ = C // PIECE
WORDS = G * P
DOTS, NORM = 0, 1
LATE_MEM = 5
SCALAR_HALF = (0, 1, 7)
TWICE = (4, 10)
EPS = 1e-8
TINY = 1e-34
FLOPS = 2 * 2 * H * C * W


def tile_contentaddressing_t_kernel(tc, memory, keys, betas, mask, out):
    nc = tc.nc
    mem2d = memory.flatten_outer_dims()
    keys2d = keys.flatten_outer_dims()
    mask2d = mask.flatten_outer_dims()
    out2d = out.flatten_outer_dims()

    with ExitStack() as ctx:
        const = ctx.enter_context(tc.tile_pool(name="const", bufs=1))
        natp = ctx.enter_context(tc.tile_pool(name="natp", bufs=3))
        grp = ctx.enter_context(tc.tile_pool(name="grp", bufs=1))
        memp = ctx.enter_context(tc.tile_pool(name="memp", bufs=5))
        head = ctx.enter_context(tc.tile_pool(name="head", bufs=2))
        cod = ctx.enter_context(tc.tile_pool(name="cod", bufs=2))
        psum = ctx.enter_context(tc.psum_pool(name="psum", bufs=4))
        ctx.enter_context(tc.manual_schedule())

        b_tiny = const.tile([P, 1], F32, name="b_tiny")
        nc.vector.memset(b_tiny[:], TINY)
        b_eps = const.tile([P, 1], F32, name="b_eps")
        nc.vector.memset(b_eps[:], EPS)
        warm = const.tile([P, 1], F32, name="warm")
        nc.scalar.activation(out=warm[:], in_=b_eps[:], func=AF.Sqrt, bias=b_tiny[:], scale=1.0)
        brow = const.tile([P, P], BF16, name="brow")
        nc.vector.memset(brow[:], 0.0)
        ident_f = const.tile([P, P], F32, name="ident_f")
        make_identity(nc, ident_f[:])
        ident_b = const.tile([P, P], BF16, name="ident_b")
        nc.vector.tensor_copy(out=ident_b[:], in_=ident_f[:])

        keys_nat = [const.tile([P, W], BF16, name="keys_nat%d" % t) for t in range(HT)]
        mask_nat = [const.tile([P, W], BF16, name="mask_nat%d" % t) for t in range(HT)]
        mem_nat = {}

        def load_head(dst, src, t):
            nc.sync.dma_start(out=dst[t][:], in_=src[t * P:(t + 1) * P, :])

        def load_mem(k):
            mem_nat[k] = natp.tile([P, 4, W], BF16, name="mem_nat")
            view = mem2d[k * CHUNK:(k + 1) * CHUNK, :].rearrange("(j p) w -> p j w", p=P)
            for j in (0, 2):
                nc.sync.dma_start(out=mem_nat[k][:, j:j + 2, :], in_=view[:, j:j + 2, :])

        nc.scalar.dma_start(out=brow[0:HT, :], in_=betas.rearrange("o (t p) -> (o t) p", p=P))
        for t in range(HT):
            load_head(mask_nat, mask2d, t)
        for t in (0, 1):
            load_head(keys_nat, keys2d, t)
        load_mem(0)
        load_mem(1)
        for t in (2, 3):
            load_head(keys_nat, keys2d, t)
        load_mem(2)

        beta_neg = const.tile([P, HT], F32, name="beta_neg")
        kn2 = const.tile([P, HT], F32, name="kn2")
        kn = const.tile([P, HT], F32, name="kn")
        key_codes = const.tile([P, 2 * HT * WORDS], U32, name="key_codes", align_bytes=64)
        key_scale = const.tile([P, 2 * HT * WORDS], U8, name="key_scale", align_bytes=64)
        s_all = [const.tile([P, C], F32, name="s%d" % t) for t in range(HT)]
        mem_codes = [const.tile([P, G * CHUNK], U32, name="mem_codes%d" % k, align_bytes=64) for k in range(NCH)]
        mem_scale = [const.tile([P, G * CHUNK], U8, name="mem_scale%d" % k, align_bytes=64) for k in range(NCH)]
        km, head_nat, head_t, head_grp = {}, {}, {}, {}
        mem_t, mem_grp, sq_grp, sq_codes = {}, {}, {}, {}

        def t_bank(shape):
            return psum.tile(shape, F32, name="tbank", tag="T")

        def acc_bank(shape):
            return psum.tile(shape, F32, name="acc", tag="acc")

        def mask_square(t):
            m2 = head_nat[t, NORM] = head.tile([P, W], BF16, name="m2")
            m = mask_nat[t][:]
            nc.vector.tensor_tensor(out=m2[:], in0=m, in1=m, op=ALU.mult)

        def key_mask(t):
            km[t] = head.tile([P, W], F32, name="km")
            nc.vector.tensor_tensor(out=km[t][:], in0=keys_nat[t][:], in1=mask_nat[t][:], op=ALU.mult)

        def key_mask2(t):
            km2 = head_nat[t, DOTS] = head.tile([P, W], BF16, name="km2")
            nc.vector.tensor_tensor(out=km2[:], in0=km[t][:], in1=mask_nat[t][:], op=ALU.mult)

        def key_norm2_scalar(t):
            unused = s_all[t][:, C - CHUNK:C].bitcast(BF16)
            nc.scalar.activation(out=unused, in_=km[t][:], func=AF.Square, accum_out=kn2[:, t:t + 1])

        def key_norm2_vector(t):
            nc.vector.scalar_tensor_tensor(out=km[t][:], in0=km[t][:], scalar=1.0, in1=km[t][:], op0=ALU.mult,
                                           op1=ALU.mult, accum_out=kn2[:, t:t + 1])

        def head_transposes(t, op):
            words = head_nat[t, op][:].bitcast(F32)
            head_t[t, op] = acc_bank([P, 2 * G, P])
            for i in range(2 * G):
                nc.tensor.transpose(out=head_t[t, op][:, i, :], in_=words[:, i * P:(i + 1) * P], identity=ident_f[:])

        def head_group(op):
            head_grp[op] = head.tile([P, HT, G, P, 4], BF16, name="head_grp", bufs=1, align_bytes=64)

        def head_evac(t, op):
            nc.scalar.copy(out=head_grp[op][:, t].bitcast(F32),
                           in_=head_t[t, op][:].rearrange("p (g u) h -> p g h u", u=2))

        def head_quant(t, n, op):
            cs = slice((op * HT + t) * WORDS, (op * HT + t + n) * WORDS)
            nc.vector.quantize_mx(out=key_codes[:, cs].bitcast(FP8X4), scales=key_scale[:, cs],
                                  in_=head_grp[op][:, t:t + n].rearrange("p t g h s -> p (t g h s)"))

        def mem_transposes(k, b):
            g, half = divmod(b, 2)
            words = mem_nat[k][:].bitcast(F32)
            bank = mem_t[k, b] = t_bank([P, 2, 256])
            for jj in range(2):
                for u in range(2):
                    i = 2 * g + u
                    nc.tensor.transpose(out=bank[:, u, jj * P:(jj + 1) * P],
                                        in_=words[:, 2 * half + jj, i * P:(i + 1) * P], identity=ident_f[:])

        def mem_evac(k, b):
            g, half = divmod(b, 2)
            if b == 0:
                mem_grp[k] = memp.tile([P, G, CHUNK, 4], BF16, name="mem_grp", align_bytes=64)
                sq_grp[k] = grp.tile([P, G, CHUNK, 4], BF16, name="sq_grp", align_bytes=64)
            nc.scalar.copy(out=mem_grp[k][:].bitcast(F32)[:, g, 256 * half:256 * half + 256, :],
                           in_=mem_t[k, b][:].rearrange("p u r -> p r u"))

        def mem_square(k):
            for g in range(G):
                m = mem_grp[k][:, g].rearrange("p c s -> p (c s)")
                nc.vector.tensor_tensor(out=sq_grp[k][:, g].rearrange("p c s -> p (c s)"), in0=m, in1=m, op=ALU.mult)

        def mem_quant(k):
            nc.vector.quantize_mx(out=mem_codes[k][:].bitcast(FP8X4), scales=mem_scale[k][:],
                                  in_=mem_grp[k][:].rearrange("p g c s -> p (g c s)"))

        def sq_quant(k):
            dat = cod.tile([P, G * CHUNK], U32, name="sq_codes", align_bytes=64)
            scl = cod.tile([P, G * CHUNK], U8, name="sq_scale", align_bytes=64)
            for g in range(G):
                gs = slice(g * CHUNK, (g + 1) * CHUNK)
                nc.vector.quantize_mx(out=dat[:, gs].bitcast(FP8X4), scales=scl[:, gs],
                                      in_=sq_grp[k][:, g].rearrange("p c s -> p (c s)"))
            sq_codes[k] = (dat, scl)

        def product(t, k, op, bank):
            dat, scl = (mem_codes[k], mem_scale[k]) if op == DOTS else sq_codes[k]
            for g in range(G):
                c0 = (op * HT + t) * WORDS + g * P
                gs = slice(g * CHUNK, (g + 1) * CHUNK)
                nc.tensor.matmul_mx(out=bank[:],
                                    lhsT=key_codes[:, c0:c0 + P].bitcast(FP8X4), lhsT_scale=key_scale[:, c0:c0 + P],
                                    rhs=dat[:, gs].bitcast(FP8X4), rhs_scale=scl[:, gs],
                                    start=(g == 0), stop=(g == G - 1))

        def cells(t, k):
            return s_all[t][:, k * CHUNK:(k + 1) * CHUNK]

        def mem_norm(t, k):
            bank = acc_bank([P, CHUNK])
            product(t, k, NORM, bank)
            nc.scalar.activation(out=cells(t, k), in_=bank[:], func=AF.Sqrt, bias=b_tiny[:], scale=1.0)

        head_group(NORM)
        for t in range(HT):
            mask_square(t)
            head_transposes(t, NORM)
            head_evac(t, NORM)
        beta_t = t_bank([P, P])[:].bitcast(BF16)
        nc.tensor.transpose(out=beta_t[:, 0:P], in_=brow[:], identity=ident_b[:])
        for b in range(3):
            mem_transposes(0, b)
        nc.vector.tensor_scalar(out=beta_neg[:], in0=beta_t[:, 0:HT], scalar1=-1.0, scalar2=None, op0=ALU.mult)
        mem_transposes(0, 3)
        key_mask(0)
        key_mask(1)
        for b in range(4):
            mem_evac(0, b)
        key_mask2(0)
        head_quant(0, 2, NORM)
        head_quant(2, 2, NORM)
        mem_square(0)
        sq_quant(0)
        for b in range(4):
            mem_transposes(1, b)
        for b in range(4):
            mem_evac(1, b)
        head_group(DOTS)
        head_transposes(0, DOTS)
        head_evac(0, DOTS)
        key_norm2_scalar(0)
        key_norm2_scalar(1)

        for k in range(NCH):
            key_tile = k // 2 if k in (2, 4, 6) else None
            if k + 3 < NCH:
                load_mem(k + 3)
            if key_tile:
                head_transposes(key_tile, DOTS)
            if k + 2 < NCH:
                for b in range(4):
                    mem_transposes(k + 2, b)
                for b in range(4):
                    mem_evac(k + 2, b)
            for t in range(HT):
                mem_norm(t, k)
            if key_tile:
                head_evac(key_tile, DOTS)
            if k == 3:
                key_norm2_scalar(2)
            if k + 1 < NCH:
                mem_square(k + 1)
                sq_quant(k + 1)
            if k in (2, 4):
                key_mask(key_tile + 1)
            if k < LATE_MEM:
                mem_quant(k)
            if k == 0:
                key_mask2(1)
            if k == 1:
                head_quant(0, 1, DOTS)
            if k in (2, 4):
                key_mask2(key_tile + 1)
        nc.scalar.activation(out=kn[:, 0:LAST], in_=kn2[:, 0:LAST], func=AF.Sqrt, bias=b_tiny[:], scale=1.0)
        for k in range(LATE_MEM, NCH):
            mem_quant(k)
        key_norm2_vector(LAST)
        head_quant(1, 1, DOTS)
        head_quant(2, 2, DOTS)

        part = [const.tile([P, NQ], F32, name="part%d" % t) for t in range(HT)]
        low = [const.tile([P, 2], F32, name="low%d" % t) for t in range(HT)]
        sums = [const.tile([P, 1], F32, name="sums%d" % t) for t in range(HT)]
        sums_a = const.tile([P, 1], F32, name="sums_a")
        fold = const.tile([P, 1], F32, name="fold")
        rs = [const.tile([P, 1], F32, name="rs%d" % t) for t in range(HT)]
        rk = const.tile([P, 1], F32, name="rk")
        rs_a = const.tile([P, 1], F32, name="rs_a")
        dots, copies = {}, {}

        def piece(i, c0=0, c1=PIECE):
            t, q = divmod(i, NQ)
            return s_all[t][:, q * PIECE + c0:q * PIECE + c1]

        def root_recip(t, c0, cn):
            cols = s_all[t][:, c0:c0 + cn]
            nc.scalar.activation(out=cols, in_=cols, func=AF.Abs_reciprocal_sqrt, bias=b_eps[:],
                                 scale=kn[:, t:t + 1])

        def scalar_square(i):
            if i in SCALAR_HALF:
                a = piece(i, 0, CHUNK)
                nc.scalar.activation(out=a, in_=a, func=AF.Square)

        def gpsimd_square(i):
            if i not in TWICE:
                a = piece(i, CHUNK if i in SCALAR_HALF else 0)
                nc.gpsimd.tensor_tensor(out=a, in0=a, in1=a, op=ALU.mult)

        def dots_product(t, k):
            dots[t, k] = acc_bank([P, CHUNK]) if k % 2 == 0 else t_bank([P, CHUNK])
            product(t, k, DOTS, dots[t, k])

        def recip_copy(t, k):
            copies[t, k] = t_bank([P, CHUNK]) if k % 2 == 0 else acc_bank([P, CHUNK])
            nc.tensor.matmul(out=copies[t, k][:], lhsT=ident_f[:], rhs=cells(t, k), start=True, stop=True)

        def score(t, k):
            nc.vector.scalar_tensor_tensor(out=cells(t, k), in0=dots[t, k][:], scalar=beta_neg[:, t:t + 1],
                                           in1=cells(t, k), op0=ALU.mult, op1=ALU.mult)

        def second_factor(t, k):
            nc.vector.scalar_tensor_tensor(out=cells(t, k), in0=copies[t, k][:], scalar=1.0, in1=cells(t, k),
                                           op0=ALU.mult, op1=ALU.mult)

        def part_min(t, i, c0, cn):
            cols = s_all[t][:, c0:c0 + cn]
            nc.vector.tensor_scalar(out=cols, in0=cols, scalar1=1.0, scalar2=None, op0=ALU.mult, op1=ALU.min,
                                    accum_out=part[t][:, i:i + 1])

        def row_min(t, col, n):
            nc.vector.tensor_reduce(out=low[t][:, col:col + 1], in_=part[t][:, 0:n], axis=AX.X, op=ALU.min)

        def row_exp(t, c0, cn, col, total):
            cols = s_all[t][:, c0:c0 + cn]
            nc.scalar.activation(out=cols, in_=cols, func=AF.Exp, bias=low[t][:, col:col + 1], scale=-1.0,
                                 accum_out=total[:])

        def row_recip(t):
            nc.vector.reciprocal(out=rs[t][:], in_=sums[t][:])

        def scale_store(t, c0, cn, eng, by):
            cols = s_all[t][:, c0:c0 + cn]
            if eng == "v":
                nc.vector.tensor_scalar(out=cols, in0=cols, scalar1=by[:], scalar2=None, op0=ALU.mult)
            elif eng == "s":
                nc.scalar.activation(out=cols, in_=cols, func=AF.Copy, scale=by[:])
            else:
                nc.gpsimd.tensor_scalar(out=cols, in0=cols, scalar1=by[:], scalar2=0.0, op0=ALU.mult, op1=ALU.add)
            nc.sync.dma_start(out=out2d[t * P:(t + 1) * P, c0:c0 + cn], in_=cols)

        def scale_store_row(t, engines):
            for q, eng in enumerate(engines):
                scale_store(t, q * PIECE, PIECE, eng, rs[t])

        for i in range(HT * NQ):
            t, q = divmod(i, NQ)
            if i < 2:
                root_recip(t, q * PIECE, CHUNK)
                root_recip(t, q * PIECE + CHUNK, CHUNK)
                scalar_square(i)
            elif q % 2 == 0:
                if t == LAST - 1 and q == 0:
                    nc.scalar.activation(out=rk[:], in_=kn2[:, LAST:HT], func=AF.Abs_reciprocal_sqrt,
                                         bias=b_tiny[:], scale=1.0)
                if t == LAST - 1 and q == 2:
                    nc.scalar.activation(out=kn[:, LAST:HT], in_=kn2[:, LAST:HT], func=AF.Copy, scale=rk[:])
                if i == 2:
                    root_recip(t, q * PIECE, PIECE)
                    root_recip(t, (q + 1) * PIECE, PIECE)
                else:
                    root_recip(t, q * PIECE, 2 * PIECE)
                scalar_square(i)
                scalar_square(i + 1)
            gpsimd_square(i)

        for t in range(HT):
            for q in range(NQ):
                dots_product(t, 2 * q)
                dots_product(t, 2 * q + 1)
                if t * NQ + q in TWICE:
                    recip_copy(t, 2 * q)
                    recip_copy(t, 2 * q + 1)
                score(t, 2 * q)
                if q == 0 and t >= 1:
                    part_min(t - 1, 1, HALF, HALF)
                if q == 2:
                    part_min(t, 0, 0, HALF)
                if q == 3 and t == LAST:
                    part_min(t, 1, HALF, PIECE)
                score(t, 2 * q + 1)
                if t * NQ + q in TWICE:
                    second_factor(t, 2 * q)
                    second_factor(t, 2 * q + 1)
                if q == 0 and t >= 1:
                    row_min(t - 1, 0, 2)
                    if t != 2:
                        row_exp(t - 1, 0, C, 0, sums[t - 1])
                if t == 2 and q == 1:
                    row_recip(0)
                    scale_store_row(0, "ssss")
                    row_exp(1, 0, C, 0, sums[1])
                if t == LAST and q == 1:
                    row_recip(1)
                    scale_store_row(1, "gggg")
                if t == LAST and q == 2:
                    row_min(t, 0, 1)
                    row_recip(2)
                    row_exp(t, 0, HALF, 0, sums_a)
        part_min(LAST, 2, C - PIECE, CHUNK)
        part_min(LAST, 3, C - CHUNK, CHUNK)
        row_min(LAST, 1, NQ)
        scale_store_row(2, "ggvv")

        nc.scalar.activation(out=fold[:], in_=low[LAST][:, 0:1], func=AF.Exp, bias=low[LAST][:, 1:2], scale=-1.0)
        row_exp(LAST, HALF, HALF, 1, sums[LAST])
        nc.vector.scalar_tensor_tensor(out=sums[LAST][:], in0=sums_a[:], scalar=fold[:], in1=sums[LAST][:],
                                       op0=ALU.mult, op1=ALU.add)
        row_recip(LAST)
        scale_store(LAST, HALF, CHUNK, "v", rs[LAST])
        nc.vector.tensor_tensor(out=rs_a[:], in0=rs[LAST][:], in1=fold[:], op=ALU.mult)
        scale_store(LAST, HALF + CHUNK, CHUNK, "v", rs[LAST])
        scale_store(LAST, HALF + PIECE, PIECE, "v", rs[LAST])
        scale_store(LAST, 0, PIECE, "v", rs_a)
        scale_store(LAST, PIECE, PIECE, "v", rs_a)
